import numpy as np
import ml_dtypes


def mxq(x, axis, fmt="e4m3"):
    dtype, down = {"e4m3": (ml_dtypes.float8_e4m3fn, 7), "e5m2": (ml_dtypes.float8_e5m2, 14)}[fmt]
    v = np.moveaxis(np.asarray(x, np.float32).astype(ml_dtypes.bfloat16).astype(np.float64), axis, -1)
    blocks = v.reshape(v.shape[:-1] + (-1, 32))
    amax = np.abs(blocks).max(-1, keepdims=True)
    byte = np.maximum(np.where(amax > 0, np.frexp(amax)[1] - 1 + 127, 0) - down, 1)
    scale = np.exp2(byte - 127.0)
    codes = (blocks / scale).astype(np.float32).astype(dtype).astype(np.float64)
    return np.moveaxis((codes * scale).reshape(v.shape), -1, axis)


WIDE = False


def mx_kscale(k):
    if not WIDE:
        return np.ones(k)
    levels = np.array([10, -10, 5, -5, 0])
    a = np.random.permutation(np.resize(levels, k // 512 * 4)).reshape(k // 512, 4)
    idx = np.arange(k)
    return np.exp2(a[idx // 512, idx % 128 // 32])


BF16 = ml_dtypes.bfloat16


def bf(x):
    return np.asarray(x, np.float32).astype(BF16)


def f64(x):
    return np.asarray(x).astype(np.float64)


B, F, N, D, HID, CELL, BUF = 16, 16, 16, 64, 512, 2048, 1536


def erf(v):
    a = np.minimum(np.abs(v), 6.0)
    a2 = a * a
    term = a.copy()
    total = a.copy()
    for n in range(1, 100):
        term = term * (a2 / (n + 0.5))
        total = total + term
    return np.sign(v) * (2.0 / np.sqrt(np.pi)) * np.exp(-a2) * total


def gelu(v):
    return 0.5 * v * (1.0 + erf(v / np.sqrt(2.0)))


def elu(v):
    return np.where(v > 0.0, v, np.exp(np.minimum(v, 0.0)) - 1.0)


def setup_inputs():
    s = mx_kscale(D * F)
    c = mx_kscale(CELL)
    zs = s.reshape(D, F).T[None, :, None, :]
    rows = np.concatenate([c, np.ones(BUF)])
    return {"z": bf(np.random.standard_normal((B, F, N, D)) * zs),
            "cells": bf(np.random.standard_normal((B, N, CELL)) * c),
            "buf_W": bf(np.random.standard_normal((F * D, BUF)) / np.sqrt(F * D) / s[:, None]),
            "buf_b": bf(np.random.standard_normal(BUF) * 0.3),
            "lam_W1": bf(np.random.standard_normal((CELL + BUF, HID)) / np.sqrt(CELL + BUF) / rows[:, None]),
            "lam_b1": bf(np.random.standard_normal(HID) * 0.3)}


def reference(z, cells, buf_W, buf_b, lam_W1, lam_b1):
    zt = f64(z).transpose(0, 2, 3, 1).reshape(B, N, D * F)
    z_b = elu((mxq(zt, 2, "e4m3") @ mxq(f64(buf_W), 0, "e4m3")) + f64(buf_b))
    w = f64(lam_W1)
    p = mxq(f64(cells), 2, "e4m3") @ mxq(w[:CELL], 0, "e4m3")
    q = mxq(z_b, 2, "e4m3") @ mxq(w[CELL:], 0, "e4m3")
    return gelu(p[:, :, None, :] + q[:, None, :, :] + f64(lam_b1))

@@ -1,0 +1,302 @@
+from contextlib import ExitStack
+
+import concourse.mybir as mybir
+from concourse.masks import make_identity
+
+BF16 = mybir.dt.bfloat16
+F32 = mybir.dt.float32
+U32 = mybir.dt.uint32
+U8 = mybir.dt.uint8
+FP8X4 = mybir.dt.float8_e4m3fn_x4
+ACT = mybir.ActivationFunctionType
+ALU = mybir.AluOpType
+
+P = 128
+PACK = 4
+K_PASS = P * PACK
+
+B, F, N, D, HID, CELL, BUF = 16, 16, 16, 64, 512, 2048, 1536
+M = B * N
+K_Z = D * F
+Z_PASSES = K_Z // K_PASS
+CELL_PASSES = CELL // K_PASS
+BUF_PASSES = BUF // K_PASS
+UNIT_COLS = 512
+HID_CHUNKS = HID // P
+M_TILES = M // P
+SCALAR_UNITS_OF_FIVE = (1, 3)
+GROUP_BATCHES = 2
+GROUP_ROWS = GROUP_BATCHES * N * N
+GROUP_TILES = GROUP_ROWS // P
+
+FLOPS = 2 * M * (K_Z * BUF + CELL * HID + BUF * HID)
+
+
+def tile_interaction_net_pa_kernel(tc, z, cells, buf_W, buf_b, lam_W1, lam_b1, out):
+    nc = tc.nc
+    with ExitStack() as stack:
+        const = stack.enter_context(tc.tile_pool(name="const", bufs=1))
+        raws = stack.enter_context(tc.tile_pool(name="raws", bufs=1))
+        keep = stack.enter_context(tc.tile_pool(name="keep", bufs=1))
+        stage = stack.enter_context(tc.tile_pool(name="stage", bufs=3))
+        psum = stack.enter_context(tc.psum_pool(name="psum", bufs=6))
+        psum_q = stack.enter_context(tc.psum_pool(name="psum_q", bufs=2))
+        stack.enter_context(tc.manual_schedule())
+
+        ident_bf = const.tile([P, P], BF16)
+        make_identity(nc, ident_bf[:])
+        ident_f32 = const.tile([P, P], F32)
+        make_identity(nc, ident_f32[:])
+        bias_rows = const.tile([P, P], BF16)
+        nc.vector.memset(bias_rows[:], 0.0)
+        warm = const.tile([P, 4], F32)
+        nc.vector.memset(warm[:], 0.0)
+
+        n_buf_rows = BUF // P
+        nc.gpsimd.dma_start(out=bias_rows[0:n_buf_rows, :], in_=buf_b.rearrange("(r c) -> r c", c=P))
+        nc.gpsimd.dma_start(
+            out=bias_rows[n_buf_rows : n_buf_rows + HID_CHUNKS, :], in_=lam_b1.rearrange("(r c) -> r c", c=P)
+        )
+        nc.scalar.activation(out=warm[:, 1:2], in_=warm[:, 0:1], func=ACT.Exp)
+
+        x_sb = [raws.tile([P, F, D], BF16, name="x_sb%d" % mt) for mt in range(M_TILES)]
+        raw_units = []
+        for cb in range(BUF_PASSES):
+            for g in range(Z_PASSES):
+                raw = raws.tile([P, PACK, UNIT_COLS], BF16, name="raw_buf%d_%d" % (cb, g))
+                nc.sync.dma_start(
+                    out=raw[:],
+                    in_=buf_W[K_PASS * g : K_PASS * (g + 1), UNIT_COLS * cb : UNIT_COLS * (cb + 1)].rearrange(
+                        "(p t) w -> p t w", t=PACK
+                    ),
+                )
+                raw_units.append(raw)
+            if cb == 0:
+                with nc.allow_non_contiguous_dma(reason="z rows of 64 features are 128-byte runs"):
+                    for b in range(B):
+                        mt, b_lo = divmod(b, B // M_TILES)
+                        nc.sync.dma_start(
+                            out=x_sb[mt][N * b_lo : N * b_lo + N, :, :],
+                            in_=z[b, :, :, :].rearrange("f n d -> n f d"),
+                        )
+        cells_rows = cells.rearrange("b n k -> (b n) k")
+        c_sb = []
+        for mt in range(M_TILES):
+            c_tile = raws.tile([P, CELL], BF16, name="c_sb%d" % mt)
+            nc.sync.dma_start(out=c_tile[:], in_=cells_rows[P * mt : P * (mt + 1), :])
+            c_sb.append(c_tile)
+        for g in range(BUF_PASSES):
+            raw = raws.tile([P, PACK, UNIT_COLS], BF16, name="raw_bot%d" % g)
+            nc.sync.dma_start(
+                out=raw[:],
+                in_=lam_W1[CELL + K_PASS * g : CELL + K_PASS * (g + 1), :].rearrange("(t p) w -> p t w", p=P),
+            )
+            raw_units.append(raw)
+        for g in range(CELL_PASSES):
+            raw = raws.tile([P, PACK, UNIT_COLS], BF16, name="raw_top%d" % g)
+            for u in range(2):
+                row0 = K_PASS * g + 2 * P * u
+                nc.sync.dma_start(
+                    out=raw[:, 2 * u : 2 * u + 2, :],
+                    in_=lam_W1[row0 : row0 + 2 * P, :].rearrange("(p e) w -> p e w", e=2),
+                )
+            raw_units.append(raw)
+
+        unit_codes = []
+        unit_scales = []
+        for i in range(len(raw_units)):
+            unit_codes.append(keep.tile([P, UNIT_COLS], U32, name="unit_codes%d" % i, align_bytes=64))
+            unit_scales.append(keep.tile([P, UNIT_COLS], U8, name="unit_scales%d" % i, align_bytes=64))
+
+        def regroup_unit(i):
+            grouped = stage.tile([P, UNIT_COLS, PACK], BF16, name="grouped_w", align_bytes=64)
+            src = raw_units[i][:].rearrange("p t (c i) -> p c t i", i=4)
+            dst = grouped[:].rearrange("p (c i) t -> p c t i", i=4)
+            if i % 5 in SCALAR_UNITS_OF_FIVE:
+                nc.scalar.copy(out=dst, in_=src)
+            else:
+                nc.vector.tensor_copy(out=dst, in_=src)
+            return grouped
+
+        def quantise_unit(i, grouped):
+            nc.vector.quantize_mx(
+                out=unit_codes[i][:].bitcast(FP8X4),
+                scales=unit_scales[i][:],
+                in_=grouped[:].rearrange("p w t -> p (w t)"),
+            )
+
+        def quantise_rows(name, grouped_flat):
+            codes = keep.tile([P, M], U32, name=name + "_codes", align_bytes=64)
+            scales = keep.tile([P, M], U8, name=name + "_scales", align_bytes=64)
+            nc.vector.quantize_mx(out=codes[:].bitcast(FP8X4), scales=scales[:], in_=grouped_flat)
+            return codes, scales
+
+        def mx_group(acc, weights, col0, rows):
+            n_pass = len(weights)
+            for g in range(n_pass):
+                nc.tensor.matmul_mx(
+                    out=acc,
+                    lhsT=unit_codes[weights[g]][:, col0 : col0 + P].bitcast(FP8X4),
+                    lhsT_scale=unit_scales[weights[g]][:, col0 : col0 + P],
+                    rhs=rows[g][0][:].bitcast(FP8X4),
+                    rhs_scale=rows[g][1][:],
+                    start=(g == 0),
+                    stop=(g == n_pass - 1),
+                )
+
+        bias_ps = psum.tile([P, P], BF16, name="bias_ps", tag="bank")
+        nc.tensor.transpose(bias_ps[:], bias_rows[:], ident_bf[:])
+        bias = const.tile([P, n_buf_rows + HID_CHUNKS], F32)
+        nc.vector.tensor_copy(out=bias[:], in_=bias_ps[:, 0 : n_buf_rows + HID_CHUNKS])
+
+        pair = [regroup_unit(0), regroup_unit(1)]
+        x_perm = []
+        for mt in range(M_TILES):
+            xp = raws.tile([P, Z_PASSES, PACK, P], BF16, name="x_perm%d" % mt)
+            for g in range(Z_PASSES):
+                nc.vector.tensor_copy(
+                    out=xp[:, g, :, :].rearrange("m t (dp fh) -> m t dp fh", fh=F // PACK),
+                    in_=x_sb[mt][:, :, (D // Z_PASSES) * g : (D // Z_PASSES) * (g + 1)].rearrange(
+                        "m (fh t) dp -> m t dp fh", t=PACK
+                    ),
+                )
+            x_perm.append(xp)
+        quantise_unit(0, pair[0])
+        quantise_unit(1, pair[1])
+        zt_q = []
+        for g in range(Z_PASSES):
+            zt_ps = psum.tile([P, PACK, M], BF16, name="zt_ps", tag="bank")
+            for t in range(PACK):
+                for mt in range(M_TILES):
+                    nc.tensor.transpose(zt_ps[:, t, P * mt : P * (mt + 1)], x_perm[mt][:, g, t, :], ident_bf[:])
+            grouped = stage.tile([P, M, PACK], BF16, name="grouped_a", align_bytes=64)
+            nc.scalar.copy(out=grouped[:], in_=zt_ps[:].rearrange("p t m -> p m t"))
+            zt_q.append(quantise_rows("zt%d" % g, grouped[:].rearrange("p m t -> p (m t)")))
+
+        zb_q = []
+        elu_parts = []
+
+        def finish_elu(g2):
+            v_sb, e_sb = elu_parts[g2]
+            nc.vector.tensor_scalar(out=e_sb[:], in0=e_sb[:], scalar1=-1.0, scalar2=0.0, op0=ALU.add, op1=ALU.min)
+            grouped = stage.tile([P, M, PACK], BF16, name="grouped_a", align_bytes=64)
+            nc.vector.tensor_tensor(
+                out=grouped[:],
+                in0=v_sb[:].rearrange("p t m -> p m t"),
+                in1=e_sb[:].rearrange("p t m -> p m t"),
+                op=ALU.max,
+            )
+            return grouped
+
+        for g2 in range(BUF_PASSES):
+            pair = [regroup_unit(2 * g2 + 2), regroup_unit(2 * g2 + 3)]
+            v_sb = stage.tile([P, PACK, M], F32, name="v_sb")
+            for half in range(2):
+                acc = psum.tile([P, 2, M], F32, name="zb_ps", tag="bank")
+                for s in range(2):
+                    t = 2 * half + s
+                    mx_group(acc[:, s, :], [2 * g2, 2 * g2 + 1], P * t, zt_q)
+                    nc.scalar.activation(
+                        out=v_sb[:, t, :],
+                        in_=acc[:, s, :],
+                        func=ACT.Identity,
+                        bias=bias[:, PACK * g2 + t : PACK * g2 + t + 1],
+                        scale=1.0,
+                    )
+            e_sb = stage.tile([P, PACK, M], F32, name="e_sb")
+            nc.scalar.activation(out=e_sb[:], in_=v_sb[:], func=ACT.Exp)
+            elu_parts.append((v_sb, e_sb))
+            if g2 > 0:
+                grouped = finish_elu(g2 - 1)
+            quantise_unit(2 * g2 + 2, pair[0])
+            quantise_unit(2 * g2 + 3, pair[1])
+            if g2 > 0:
+                zb_q.append(quantise_rows("zb%d" % (g2 - 1), grouped[:].rearrange("p m t -> p (m t)")))
+
+        waiting = regroup_unit(8)
+        cells_grouped = []
+        for g in range(CELL_PASSES):
+            c_ps = psum.tile([P, 2, M], F32, name="c_ps", tag="bank")
+            for u in range(2):
+                for mt in range(M_TILES):
+                    word0 = (K_PASS // 2) * g + P * u
+                    nc.tensor.transpose(
+                        c_ps[:, u, P * mt : P * (mt + 1)], c_sb[mt][:].bitcast(F32)[:, word0 : word0 + P], ident_f32[:]
+                    )
+            grouped = stage.tile([P, M * PACK], BF16, name="grouped_c", bufs=CELL_PASSES, align_bytes=64)
+            nc.scalar.copy(
+                out=grouped[:].bitcast(F32).rearrange("p (m u) -> p m u", u=2), in_=c_ps[:].rearrange("p u m -> p m u")
+            )
+            cells_grouped.append(grouped)
+        grouped = finish_elu(BUF_PASSES - 1)
+        quantise_unit(8, waiting)
+        zb_q.append(quantise_rows("zb%d" % (BUF_PASSES - 1), grouped[:].rearrange("p m t -> p (m t)")))
+        q_ps = []
+        for half in range(2):
+            acc = psum_q.tile([P, 2, M], F32, name="q_ps")
+            for s in range(2):
+                mx_group(acc[:, s, :], [6, 7, 8], P * (2 * half + s), zb_q)
+            q_ps.append(acc)
+        cells_q = [quantise_rows("cells%d" % g, cells_grouped[g][:]) for g in range(CELL_PASSES)]
+
+        p_ps = [psum.tile([P, M], F32, name="p_ps%d" % c, tag="bank") for c in range(HID_CHUNKS)]
+
+        def p_passes(g):
+            for c in range(HID_CHUNKS):
+                nc.tensor.matmul_mx(
+                    out=p_ps[c][:],
+                    lhsT=unit_codes[9 + g][:, P * c : P * (c + 1)].bitcast(FP8X4),
+                    lhsT_scale=unit_scales[9 + g][:, P * c : P * (c + 1)],
+                    rhs=cells_q[g][0][:].bitcast(FP8X4),
+                    rhs_scale=cells_q[g][1][:],
+                    start=(g == 0),
+                    stop=(g == CELL_PASSES - 1),
+                )
+
+        waiting = regroup_unit(9)
+        for g in range(1, CELL_PASSES):
+            grouped = regroup_unit(9 + g)
+            quantise_unit(9 + g - 1, waiting)
+            p_passes(g - 1)
+            waiting = grouped
+        quantise_unit(12, waiting)
+        p_passes(CELL_PASSES - 1)
+        p_sb = keep.tile([P, HID_CHUNKS, M], F32)
+        for c in range(HID_CHUNKS):
+            nc.scalar.activation(
+                out=p_sb[:, c, :],
+                in_=p_ps[c][:],
+                func=ACT.Identity,
+                bias=bias[:, n_buf_rows + c : n_buf_rows + c + 1],
+                scale=1.0,
+            )
+        nc.scalar.activation(out=warm[:, 3:4], in_=warm[:, 2:3], func=ACT.Gelu)
+
+        out_rows = out.rearrange("b i j h -> (b i j) h")
+        for grp in range(B // GROUP_BATCHES):
+            m0 = GROUP_BATCHES * N * grp
+            m1 = m0 + GROUP_BATCHES * N
+            sums = stage.tile([P, HID_CHUNKS, GROUP_ROWS], F32, name="sums")
+            for c in range(HID_CHUNKS):
+                nc.vector.tensor_tensor(
+                    out=sums[:, c, :].rearrange("p (b i j) -> p b i j", i=N, j=N),
+                    in0=q_ps[c // 2][:, c % 2, m0:m1]
+                    .rearrange("p (b j) -> p b j", j=N)
+                    .unsqueeze(2)
+                    .to_broadcast([P, GROUP_BATCHES, N, N]),
+                    in1=p_sb[:, c, m0:m1]
+                    .rearrange("p (b i) -> p b i", i=N)
+                    .unsqueeze(3)
+                    .to_broadcast([P, GROUP_BATCHES, N, N]),
+                    op=ALU.add,
+                )
+            o_sb = stage.tile([P, GROUP_TILES, HID], F32, name="o_sb")
+            for r in range(GROUP_TILES):
+                o_ps = psum.tile([P, HID], F32, name="o_ps", tag="bank")
+                for c in range(HID_CHUNKS):
+                    nc.tensor.transpose(o_ps[:, P * c : P * (c + 1)], sums[:, c, P * r : P * (r + 1)], ident_f32[:])
+                nc.scalar.activation(out=o_sb[:, r, :], in_=o_ps[:], func=ACT.Gelu)
+            nc.sync.dma_start(
+                out=out_rows[GROUP_ROWS * grp : GROUP_ROWS * (grp + 1), :].rearrange("(r p) h -> p r h", p=P),
+                in_=o_sb[:],
+            )

@@ -24,7 +24,6 @@ BUF_PASSES = BUF // K_PASS
 UNIT_COLS = 512
 HID_CHUNKS = HID // P
 M_TILES = M // P
-SCALAR_UNITS_OF_FIVE = (1, 3)
 GROUP_BATCHES = 2
 GROUP_ROWS = GROUP_BATCHES * N * N
 GROUP_TILES = GROUP_ROWS // P
@@ -39,8 +38,8 @@ def tile_interaction_net_pa_kernel(tc, z, cells, buf_W, buf_b, lam_W1, lam_b1, o
         raws = stack.enter_context(tc.tile_pool(name="raws", bufs=1))
         keep = stack.enter_context(tc.tile_pool(name="keep", bufs=1))
         stage = stack.enter_context(tc.tile_pool(name="stage", bufs=3))
-        psum = stack.enter_context(tc.psum_pool(name="psum", bufs=6))
-        psum_q = stack.enter_context(tc.psum_pool(name="psum_q", bufs=2))
+        psum = stack.enter_context(tc.psum_pool(name="psum", bufs=4))
+        psum_p = stack.enter_context(tc.psum_pool(name="psum_p", bufs=1))
         stack.enter_context(tc.manual_schedule())
 
         ident_bf = const.tile([P, P], BF16)
@@ -71,13 +70,12 @@ def tile_interaction_net_pa_kernel(tc, z, cells, buf_W, buf_b, lam_W1, lam_b1, o
                     ),
                 )
                 raw_units.append(raw)
-            if cb == 0:
+            if cb < M_TILES:
                 with nc.allow_non_contiguous_dma(reason="z rows of 64 features are 128-byte runs"):
-                    for b in range(B):
-                        mt, b_lo = divmod(b, B // M_TILES)
+                    for b_lo in range(B // M_TILES):
                         nc.sync.dma_start(
-                            out=x_sb[mt][N * b_lo : N * b_lo + N, :, :],
-                            in_=z[b, :, :, :].rearrange("f n d -> n f d"),
+                            out=x_sb[cb][N * b_lo : N * b_lo + N, :, :],
+                            in_=z[(B // M_TILES) * cb + b_lo, :, :, :].rearrange("f n d -> n f d"),
                         )
         cells_rows = cells.rearrange("b n k -> (b n) k")
         c_sb = []
@@ -108,11 +106,11 @@ def tile_interaction_net_pa_kernel(tc, z, cells, buf_W, buf_b, lam_W1, lam_b1, o
             unit_codes.append(keep.tile([P, UNIT_COLS], U32, name="unit_codes%d" % i, align_bytes=64))
             unit_scales.append(keep.tile([P, UNIT_COLS], U8, name="unit_scales%d" % i, align_bytes=64))
 
-        def regroup_unit(i):
+        def regroup_unit(i, on_scalar):
             grouped = stage.tile([P, UNIT_COLS, PACK], BF16, name="grouped_w", align_bytes=64)
             src = raw_units[i][:].rearrange("p t (c i) -> p c t i", i=4)
             dst = grouped[:].rearrange("p (c i) t -> p c t i", i=4)
-            if i % 5 in SCALAR_UNITS_OF_FIVE:
+            if on_scalar:
                 nc.scalar.copy(out=dst, in_=src)
             else:
                 nc.vector.tensor_copy(out=dst, in_=src)
@@ -144,37 +142,67 @@ def tile_interaction_net_pa_kernel(tc, z, cells, buf_W, buf_b, lam_W1, lam_b1, o
                     stop=(g == n_pass - 1),
                 )
 
-        bias_ps = psum.tile([P, P], BF16, name="bias_ps", tag="bank")
-        nc.tensor.transpose(bias_ps[:], bias_rows[:], ident_bf[:])
-        bias = const.tile([P, n_buf_rows + HID_CHUNKS], F32)
-        nc.vector.tensor_copy(out=bias[:], in_=bias_ps[:, 0 : n_buf_rows + HID_CHUNKS])
-
-        pair = [regroup_unit(0), regroup_unit(1)]
         x_perm = []
-        for mt in range(M_TILES):
-            xp = raws.tile([P, Z_PASSES, PACK, P], BF16, name="x_perm%d" % mt)
-            for g in range(Z_PASSES):
-                nc.vector.tensor_copy(
-                    out=xp[:, g, :, :].rearrange("m t (dp fh) -> m t dp fh", fh=F // PACK),
-                    in_=x_sb[mt][:, :, (D // Z_PASSES) * g : (D // Z_PASSES) * (g + 1)].rearrange(
-                        "m (fh t) dp -> m t dp fh", t=PACK
-                    ),
-                )
-            x_perm.append(xp)
-        quantise_unit(0, pair[0])
-        quantise_unit(1, pair[1])
+        zt_grouped = []
         zt_q = []
-        for g in range(Z_PASSES):
-            zt_ps = psum.tile([P, PACK, M], BF16, name="zt_ps", tag="bank")
-            for t in range(PACK):
-                for mt in range(M_TILES):
-                    nc.tensor.transpose(zt_ps[:, t, P * mt : P * (mt + 1)], x_perm[mt][:, g, t, :], ident_bf[:])
-            grouped = stage.tile([P, M, PACK], BF16, name="grouped_a", align_bytes=64)
-            nc.scalar.copy(out=grouped[:], in_=zt_ps[:].rearrange("p t m -> p m t"))
-            zt_q.append(quantise_rows("zt%d" % g, grouped[:].rearrange("p m t -> p (m t)")))
+        bias = const.tile([P, n_buf_rows + HID_CHUNKS], F32)
+        for pair in range(BUF_PASSES):
+            even = regroup_unit(2 * pair, False)
+            odd = regroup_unit(2 * pair + 1, True)
+            quantise_unit(2 * pair, even)
+            if pair < M_TILES:
+                xp = raws.tile([P, Z_PASSES, PACK, P], BF16, name="x_perm%d" % pair)
+                for g in range(Z_PASSES):
+                    nc.vector.tensor_copy(
+                        out=xp[:, g, :, :].rearrange("m t (dp fh) -> m t dp fh", fh=F // PACK),
+                        in_=x_sb[pair][:, :, (D // Z_PASSES) * g : (D // Z_PASSES) * (g + 1)].rearrange(
+                            "m (fh t) dp -> m t dp fh", t=PACK
+                        ),
+                    )
+                x_perm.append(xp)
+            else:
+                for g in range(Z_PASSES):
+                    zt_q.append(quantise_rows("zt%d" % g, zt_grouped[g][:].rearrange("p m t -> p (m t)")))
+            quantise_unit(2 * pair + 1, odd)
+            if pair == M_TILES - 1:
+                bias_ps = psum.tile([P, P], BF16, name="bias_ps", tag="bank")
+                nc.tensor.transpose(bias_ps[:], bias_rows[:], ident_bf[:])
+                nc.vector.tensor_copy(out=bias[:], in_=bias_ps[:, 0 : n_buf_rows + HID_CHUNKS])
+                for g in range(Z_PASSES):
+                    zt_ps = psum.tile([P, PACK, M], BF16, name="zt_ps", tag="bank")
+                    for t in range(PACK):
+                        for mt in range(M_TILES):
+                            nc.tensor.transpose(
+                                zt_ps[:, t, P * mt : P * (mt + 1)], x_perm[mt][:, g, t, :], ident_bf[:]
+                            )
+                    grouped = stage.tile([P, M, PACK], BF16, name="grouped_a", align_bytes=64)
+                    nc.scalar.copy(out=grouped[:], in_=zt_ps[:].rearrange("p t m -> p m t"))
+                    zt_grouped.append(grouped)
 
-        zb_q = []
+        zb_ps = []
         elu_parts = []
+        zb_q = []
+
+        def buffer_passes(g2):
+            for half in range(2):
+                acc = psum.tile([P, 2, M], F32, name="zb_ps", tag="bank")
+                for s in range(2):
+                    mx_group(acc[:, s, :], [2 * g2, 2 * g2 + 1], P * (2 * half + s), zt_q)
+                zb_ps.append(acc)
+
+        def bias_and_exp(g2):
+            v_sb = stage.tile([P, PACK, M], F32, name="v_sb")
+            for t in range(PACK):
+                nc.scalar.activation(
+                    out=v_sb[:, t, :],
+                    in_=zb_ps[2 * g2 + t // 2][:, t % 2, :],
+                    func=ACT.Identity,
+                    bias=bias[:, PACK * g2 + t : PACK * g2 + t + 1],
+                    scale=1.0,
+                )
+            e_sb = stage.tile([P, PACK, M], F32, name="e_sb")
+            nc.scalar.activation(out=e_sb[:], in_=v_sb[:], func=ACT.Exp)
+            elu_parts.append((v_sb, e_sb))
 
         def finish_elu(g2):
             v_sb, e_sb = elu_parts[g2]
@@ -188,32 +216,20 @@ def tile_interaction_net_pa_kernel(tc, z, cells, buf_W, buf_b, lam_W1, lam_b1, o
             )
             return grouped
 
+        first_low = 2 * BUF_PASSES
+        low_grouped = []
+        buffer_passes(0)
         for g2 in range(BUF_PASSES):
-            pair = [regroup_unit(2 * g2 + 2), regroup_unit(2 * g2 + 3)]
-            v_sb = stage.tile([P, PACK, M], F32, name="v_sb")
-            for half in range(2):
-                acc = psum.tile([P, 2, M], F32, name="zb_ps", tag="bank")
-                for s in range(2):
-                    t = 2 * half + s
-                    mx_group(acc[:, s, :], [2 * g2, 2 * g2 + 1], P * t, zt_q)
-                    nc.scalar.activation(
-                        out=v_sb[:, t, :],
-                        in_=acc[:, s, :],
-                        func=ACT.Identity,
-                        bias=bias[:, PACK * g2 + t : PACK * g2 + t + 1],
-                        scale=1.0,
-                    )
-            e_sb = stage.tile([P, PACK, M], F32, name="e_sb")
-            nc.scalar.activation(out=e_sb[:], in_=v_sb[:], func=ACT.Exp)
-            elu_parts.append((v_sb, e_sb))
+            if g2 + 1 < BUF_PASSES:
+                buffer_passes(g2 + 1)
+            bias_and_exp(g2)
+            low_grouped.append(regroup_unit(first_low + g2, False))
             if g2 > 0:
                 grouped = finish_elu(g2 - 1)
-            quantise_unit(2 * g2 + 2, pair[0])
-            quantise_unit(2 * g2 + 3, pair[1])
-            if g2 > 0:
+                quantise_unit(first_low + g2 - 1, low_grouped[g2 - 1])
                 zb_q.append(quantise_rows("zb%d" % (g2 - 1), grouped[:].rearrange("p m t -> p (m t)")))
 
-        waiting = regroup_unit(8)
+        first_top = first_low + BUF_PASSES
         cells_grouped = []
         for g in range(CELL_PASSES):
             c_ps = psum.tile([P, 2, M], F32, name="c_ps", tag="bank")
@@ -228,49 +244,44 @@ def tile_interaction_net_pa_kernel(tc, z, cells, buf_W, buf_b, lam_W1, lam_b1, o
                 out=grouped[:].bitcast(F32).rearrange("p (m u) -> p m u", u=2), in_=c_ps[:].rearrange("p u m -> p m u")
             )
             cells_grouped.append(grouped)
+        top_grouped = [regroup_unit(first_top, True), regroup_unit(first_top + 1, False)]
         grouped = finish_elu(BUF_PASSES - 1)
-        quantise_unit(8, waiting)
+        quantise_unit(first_top - 1, low_grouped[BUF_PASSES - 1])
         zb_q.append(quantise_rows("zb%d" % (BUF_PASSES - 1), grouped[:].rearrange("p m t -> p (m t)")))
         q_ps = []
         for half in range(2):
-            acc = psum_q.tile([P, 2, M], F32, name="q_ps")
+            acc = psum.tile([P, 2, M], F32, name="q_ps", tag="bank")
             for s in range(2):
-                mx_group(acc[:, s, :], [6, 7, 8], P * (2 * half + s), zb_q)
+                mx_group(acc[:, s, :], [first_low + g for g in range(BUF_PASSES)], P * (2 * half + s), zb_q)
             q_ps.append(acc)
         cells_q = [quantise_rows("cells%d" % g, cells_grouped[g][:]) for g in range(CELL_PASSES)]
 
-        p_ps = [psum.tile([P, M], F32, name="p_ps%d" % c, tag="bank") for c in range(HID_CHUNKS)]
-
-        def p_passes(g):
+        p_ps = [psum_p.tile([P, M], F32, name="p_ps%d" % c) for c in range(HID_CHUNKS)]
+        q_sb = keep.tile([P, HID_CHUNKS, M], F32)
+        for g in range(CELL_PASSES):
+            if g + 2 < CELL_PASSES:
+                top_grouped.append(regroup_unit(first_top + g + 2, g % 2 == 0))
+            quantise_unit(first_top + g, top_grouped[g])
             for c in range(HID_CHUNKS):
                 nc.tensor.matmul_mx(
                     out=p_ps[c][:],
-                    lhsT=unit_codes[9 + g][:, P * c : P * (c + 1)].bitcast(FP8X4),
-                    lhsT_scale=unit_scales[9 + g][:, P * c : P * (c + 1)],
+                    lhsT=unit_codes[first_top + g][:, P * c : P * (c + 1)].bitcast(FP8X4),
+                    lhsT_scale=unit_scales[first_top + g][:, P * c : P * (c + 1)],
                     rhs=cells_q[g][0][:].bitcast(FP8X4),
                     rhs_scale=cells_q[g][1][:],
                     start=(g == 0),
                     stop=(g == CELL_PASSES - 1),
                 )
-
-        waiting = regroup_unit(9)
-        for g in range(1, CELL_PASSES):
-            grouped = regroup_unit(9 + g)
-            quantise_unit(9 + g - 1, waiting)
-            p_passes(g - 1)
-            waiting = grouped
-        quantise_unit(12, waiting)
-        p_passes(CELL_PASSES - 1)
-        p_sb = keep.tile([P, HID_CHUNKS, M], F32)
-        for c in range(HID_CHUNKS):
-            nc.scalar.activation(
-                out=p_sb[:, c, :],
-                in_=p_ps[c][:],
-                func=ACT.Identity,
-                bias=bias[:, n_buf_rows + c : n_buf_rows + c + 1],
-                scale=1.0,
-            )
-        nc.scalar.activation(out=warm[:, 3:4], in_=warm[:, 2:3], func=ACT.Gelu)
+            if g == 1:
+                for c in range(HID_CHUNKS):
+                    nc.scalar.activation(
+                        out=q_sb[:, c, :],
+                        in_=q_ps[c // 2][:, c % 2, :],
+                        func=ACT.Identity,
+                        bias=bias[:, n_buf_rows + c : n_buf_rows + c + 1],
+                        scale=1.0,
+                    )
+                nc.scalar.activation(out=warm[:, 3:4], in_=warm[:, 2:3], func=ACT.Gelu)
 
         out_rows = out.rearrange("b i j h -> (b i j) h")
         for grp in range(B // GROUP_BATCHES):
@@ -280,23 +291,21 @@ def tile_interaction_net_pa_kernel(tc, z, cells, buf_W, buf_b, lam_W1, lam_b1, o
             for c in range(HID_CHUNKS):
                 nc.vector.tensor_tensor(
                     out=sums[:, c, :].rearrange("p (b i j) -> p b i j", i=N, j=N),
-                    in0=q_ps[c // 2][:, c % 2, m0:m1]
-                    .rearrange("p (b j) -> p b j", j=N)
-                    .unsqueeze(2)
-                    .to_broadcast([P, GROUP_BATCHES, N, N]),
-                    in1=p_sb[:, c, m0:m1]
+                    in0=p_ps[c][:, m0:m1]
                     .rearrange("p (b i) -> p b i", i=N)
                     .unsqueeze(3)
                     .to_broadcast([P, GROUP_BATCHES, N, N]),
+                    in1=q_sb[:, c, m0:m1]
+                    .rearrange("p (b j) -> p b j", j=N)
+                    .unsqueeze(2)
+                    .to_broadcast([P, GROUP_BATCHES, N, N]),
                     op=ALU.add,
                 )
-            o_sb = stage.tile([P, GROUP_TILES, HID], F32, name="o_sb")
             for r in range(GROUP_TILES):
                 o_ps = psum.tile([P, HID], F32, name="o_ps", tag="bank")
                 for c in range(HID_CHUNKS):
                     nc.tensor.transpose(o_ps[:, P * c : P * (c + 1)], sums[:, c, P * r : P * (r + 1)], ident_f32[:])
-                nc.scalar.activation(out=o_sb[:, r, :], in_=o_ps[:], func=ACT.Gelu)
-            nc.sync.dma_start(
-                out=out_rows[GROUP_ROWS * grp : GROUP_ROWS * (grp + 1), :].rearrange("(r p) h -> p r h", p=P),
-                in_=o_sb[:],
-            )
+                o_sb = stage.tile([P, HID], F32, name="o_sb", bufs=6)
+                nc.scalar.activation(out=o_sb[:], in_=o_ps[:], func=ACT.Gelu)
+                row0 = GROUP_ROWS * grp + P * r
+                nc.sync.dma_start(out=out_rows[row0 : row0 + P, :], in_=o_sb[:])

@@ -43,22 +43,17 @@ def tile_interaction_net_pa_kernel(tc, z, cells, buf_W, buf_b, lam_W1, lam_b1, o
         stack.enter_context(tc.manual_schedule())
 
         ident_bf = const.tile([P, P], BF16)
-        make_identity(nc, ident_bf[:])
         ident_f32 = const.tile([P, P], F32)
-        make_identity(nc, ident_f32[:])
         bias_rows = const.tile([P, P], BF16)
         nc.vector.memset(bias_rows[:], 0.0)
         warm = const.tile([P, 4], F32)
         nc.vector.memset(warm[:], 0.0)
 
         n_buf_rows = BUF // P
-        nc.gpsimd.dma_start(out=bias_rows[0:n_buf_rows, :], in_=buf_b.rearrange("(r c) -> r c", c=P))
-        nc.gpsimd.dma_start(
-            out=bias_rows[n_buf_rows : n_buf_rows + HID_CHUNKS, :], in_=lam_b1.rearrange("(r c) -> r c", c=P)
-        )
         nc.scalar.activation(out=warm[:, 1:2], in_=warm[:, 0:1], func=ACT.Exp)
 
         x_sb = [raws.tile([P, F, D], BF16, name="x_sb%d" % mt) for mt in range(M_TILES)]
+        z_queues = [nc.sync, nc.gpsimd]
         raw_units = []
         for cb in range(BUF_PASSES):
             for g in range(Z_PASSES):
@@ -73,7 +68,7 @@ def tile_interaction_net_pa_kernel(tc, z, cells, buf_W, buf_b, lam_W1, lam_b1, o
             if cb < M_TILES:
                 with nc.allow_non_contiguous_dma(reason="z rows of 64 features are 128-byte runs"):
                     for b_lo in range(B // M_TILES):
-                        nc.sync.dma_start(
+                        z_queues[cb].dma_start(
                             out=x_sb[cb][N * b_lo : N * b_lo + N, :, :],
                             in_=z[(B // M_TILES) * cb + b_lo, :, :, :].rearrange("f n d -> n f d"),
                         )
@@ -99,6 +94,13 @@ def tile_interaction_net_pa_kernel(tc, z, cells, buf_W, buf_b, lam_W1, lam_b1, o
                     in_=lam_W1[row0 : row0 + 2 * P, :].rearrange("(p e) w -> p e w", e=2),
                 )
             raw_units.append(raw)
+
+        make_identity(nc, ident_bf[:])
+        make_identity(nc, ident_f32[:])
+        nc.gpsimd.dma_start(out=bias_rows[0:n_buf_rows, :], in_=buf_b.rearrange("(r c) -> r c", c=P))
+        nc.gpsimd.dma_start(
+            out=bias_rows[n_buf_rows : n_buf_rows + HID_CHUNKS, :], in_=lam_b1.rearrange("(r c) -> r c", c=P)
+        )
 
         unit_codes = []
         unit_scales = []
@@ -244,7 +246,7 @@ def tile_interaction_net_pa_kernel(tc, z, cells, buf_W, buf_b, lam_W1, lam_b1, o
                 out=grouped[:].bitcast(F32).rearrange("p (m u) -> p m u", u=2), in_=c_ps[:].rearrange("p u m -> p m u")
             )
             cells_grouped.append(grouped)
-        top_grouped = [regroup_unit(first_top, True), regroup_unit(first_top + 1, False)]
+        top_grouped = [regroup_unit(first_top, True), regroup_unit(first_top + 1, True)]
         grouped = finish_elu(BUF_PASSES - 1)
         quantise_unit(first_top - 1, low_grouped[BUF_PASSES - 1])
         zb_q.append(quantise_rows("zb%d" % (BUF_PASSES - 1), grouped[:].rearrange("p m t -> p (m t)")))
@@ -260,7 +262,7 @@ def tile_interaction_net_pa_kernel(tc, z, cells, buf_W, buf_b, lam_W1, lam_b1, o
         q_sb = keep.tile([P, HID_CHUNKS, M], F32)
         for g in range(CELL_PASSES):
             if g + 2 < CELL_PASSES:
-                top_grouped.append(regroup_unit(first_top + g + 2, g % 2 == 0))
+                top_grouped.append(regroup_unit(first_top + g + 2, g + 3 < CELL_PASSES))
             quantise_unit(first_top + g, top_grouped[g])
             for c in range(HID_CHUNKS):
                 nc.tensor.matmul_mx(
@@ -305,7 +307,7 @@ def tile_interaction_net_pa_kernel(tc, z, cells, buf_W, buf_b, lam_W1, lam_b1, o
                 o_ps = psum.tile([P, HID], F32, name="o_ps", tag="bank")
                 for c in range(HID_CHUNKS):
                     nc.tensor.transpose(o_ps[:, P * c : P * (c + 1)], sums[:, c, P * r : P * (r + 1)], ident_f32[:])
-                o_sb = stage.tile([P, HID], F32, name="o_sb", bufs=6)
+                o_sb = stage.tile([P, HID], F32, name="o_sb", bufs=10)
                 nc.scalar.activation(out=o_sb[:], in_=o_ps[:], func=ACT.Gelu)
                 row0 = GROUP_ROWS * grp + P * r
                 nc.sync.dma_start(out=out_rows[row0 : row0 + P, :], in_=o_sb[:])

@@ -50,10 +50,8 @@ def tile_interaction_net_pa_kernel(tc, z, cells, buf_W, buf_b, lam_W1, lam_b1, o
         nc.vector.memset(warm[:], 0.0)
 
         n_buf_rows = BUF // P
-        nc.scalar.activation(out=warm[:, 1:2], in_=warm[:, 0:1], func=ACT.Exp)
-
         x_sb = [raws.tile([P, F, D], BF16, name="x_sb%d" % mt) for mt in range(M_TILES)]
-        z_queues = [nc.sync, nc.gpsimd]
+        z_queues = [nc.sync, nc.scalar]
         raw_units = []
         for cb in range(BUF_PASSES):
             for g in range(Z_PASSES):
@@ -65,12 +63,12 @@ def tile_interaction_net_pa_kernel(tc, z, cells, buf_W, buf_b, lam_W1, lam_b1, o
                     ),
                 )
                 raw_units.append(raw)
-            if cb < M_TILES:
+            if cb == 0:
                 with nc.allow_non_contiguous_dma(reason="z rows of 64 features are 128-byte runs"):
-                    for b_lo in range(B // M_TILES):
-                        z_queues[cb].dma_start(
-                            out=x_sb[cb][N * b_lo : N * b_lo + N, :, :],
-                            in_=z[(B // M_TILES) * cb + b_lo, :, :, :].rearrange("f n d -> n f d"),
+                    for b in range(B):
+                        mt, b_lo = divmod(b, B // M_TILES)
+                        z_queues[b % 2].dma_start(
+                            out=x_sb[mt][N * b_lo : N * b_lo + N, :, :], in_=z[b, :, :, :].rearrange("f n d -> n f d")
                         )
         cells_rows = cells.rearrange("b n k -> (b n) k")
         c_sb = []
@@ -95,6 +93,7 @@ def tile_interaction_net_pa_kernel(tc, z, cells, buf_W, buf_b, lam_W1, lam_b1, o
                 )
             raw_units.append(raw)
 
+        nc.scalar.activation(out=warm[:, 1:2], in_=warm[:, 0:1], func=ACT.Exp)
         make_identity(nc, ident_bf[:])
         make_identity(nc, ident_f32[:])
         nc.gpsimd.dma_start(out=bias_rows[0:n_buf_rows, :], in_=buf_b.rearrange("(r c) -> r c", c=P))
@@ -144,29 +143,27 @@ def tile_interaction_net_pa_kernel(tc, z, cells, buf_W, buf_b, lam_W1, lam_b1, o
                     stop=(g == n_pass - 1),
                 )
 
-        x_perm = []
         zt_grouped = []
         zt_q = []
         bias = const.tile([P, n_buf_rows + HID_CHUNKS], F32)
         for pair in range(BUF_PASSES):
             even = regroup_unit(2 * pair, False)
-            odd = regroup_unit(2 * pair + 1, True)
+            odd = regroup_unit(2 * pair + 1, pair > 0)
             quantise_unit(2 * pair, even)
-            if pair < M_TILES:
-                xp = raws.tile([P, Z_PASSES, PACK, P], BF16, name="x_perm%d" % pair)
-                for g in range(Z_PASSES):
-                    nc.vector.tensor_copy(
-                        out=xp[:, g, :, :].rearrange("m t (dp fh) -> m t dp fh", fh=F // PACK),
-                        in_=x_sb[pair][:, :, (D // Z_PASSES) * g : (D // Z_PASSES) * (g + 1)].rearrange(
-                            "m (fh t) dp -> m t dp fh", t=PACK
-                        ),
-                    )
-                x_perm.append(xp)
-            else:
+            if pair == 1:
                 for g in range(Z_PASSES):
                     zt_q.append(quantise_rows("zt%d" % g, zt_grouped[g][:].rearrange("p m t -> p (m t)")))
             quantise_unit(2 * pair + 1, odd)
-            if pair == M_TILES - 1:
+            if pair == 0:
+                x_perm = [raws.tile([P, Z_PASSES, PACK, P], BF16, name="x_perm%d" % mt) for mt in range(M_TILES)]
+                for g in range(Z_PASSES):
+                    for mt in range(M_TILES):
+                        nc.vector.tensor_copy(
+                            out=x_perm[mt][:, g, :, :].rearrange("m t (dp fh) -> m t dp fh", fh=F // PACK),
+                            in_=x_sb[mt][:, :, (D // Z_PASSES) * g : (D // Z_PASSES) * (g + 1)].rearrange(
+                                "m (fh t) dp -> m t dp fh", t=PACK
+                            ),
+                        )
                 bias_ps = psum.tile([P, P], BF16, name="bias_ps", tag="bank")
                 nc.tensor.transpose(bias_ps[:], bias_rows[:], ident_bf[:])
                 nc.vector.tensor_copy(out=bias[:], in_=bias_ps[:, 0 : n_buf_rows + HID_CHUNKS])

@@ -24,6 +24,9 @@ BUF_PASSES = BUF // K_PASS
 UNIT_COLS = 512
 HID_CHUNKS = HID // P
 M_TILES = M // P
+N_HI = 2
+N_LO = N // N_HI
+F_HI = F // PACK
 GROUP_BATCHES = 2
 GROUP_ROWS = GROUP_BATCHES * N * N
 GROUP_TILES = GROUP_ROWS // P
@@ -50,8 +53,7 @@ def tile_interaction_net_pa_kernel(tc, z, cells, buf_W, buf_b, lam_W1, lam_b1, o
         nc.vector.memset(warm[:], 0.0)
 
         n_buf_rows = BUF // P
-        x_sb = [raws.tile([P, F, D], BF16, name="x_sb%d" % mt) for mt in range(M_TILES)]
-        z_queues = [nc.sync, nc.scalar]
+        x_sb = raws.tile([P, F_HI, N_LO, D], BF16)
         raw_units = []
         for cb in range(BUF_PASSES):
             for g in range(Z_PASSES):
@@ -64,11 +66,12 @@ def tile_interaction_net_pa_kernel(tc, z, cells, buf_W, buf_b, lam_W1, lam_b1, o
                 )
                 raw_units.append(raw)
             if cb == 0:
-                with nc.allow_non_contiguous_dma(reason="z rows of 64 features are 128-byte runs"):
-                    for b in range(B):
-                        mt, b_lo = divmod(b, B // M_TILES)
-                        z_queues[b % 2].dma_start(
-                            out=x_sb[mt][N * b_lo : N * b_lo + N, :, :], in_=z[b, :, :, :].rearrange("f n d -> n f d")
+                for t in range(PACK):
+                    for n_hi in range(N_HI):
+                        part0 = B * (N_HI * t + n_hi)
+                        nc.sync.dma_start(
+                            out=x_sb[part0 : part0 + B, :, :, :].rearrange("b f n d -> b f (n d)"),
+                            in_=z[:, t:F:PACK, N_LO * n_hi : N_LO * (n_hi + 1), :].rearrange("b f n d -> b f (n d)"),
                         )
         cells_rows = cells.rearrange("b n k -> (b n) k")
         c_sb = []
@@ -155,27 +158,24 @@ def tile_interaction_net_pa_kernel(tc, z, cells, buf_W, buf_b, lam_W1, lam_b1, o
                     zt_q.append(quantise_rows("zt%d" % g, zt_grouped[g][:].rearrange("p m t -> p (m t)")))
             quantise_unit(2 * pair + 1, odd)
             if pair == 0:
-                x_perm = [raws.tile([P, Z_PASSES, PACK, P], BF16, name="x_perm%d" % mt) for mt in range(M_TILES)]
+                x_perm = raws.tile([P, N_LO, Z_PASSES, P], BF16)
                 for g in range(Z_PASSES):
-                    for mt in range(M_TILES):
-                        nc.vector.tensor_copy(
-                            out=x_perm[mt][:, g, :, :].rearrange("m t (dp fh) -> m t dp fh", fh=F // PACK),
-                            in_=x_sb[mt][:, :, (D // Z_PASSES) * g : (D // Z_PASSES) * (g + 1)].rearrange(
-                                "m (fh t) dp -> m t dp fh", t=PACK
-                            ),
-                        )
+                    nc.vector.tensor_copy(
+                        out=x_perm[:, :, g, :].rearrange("q n (d f) -> q n d f", f=F_HI),
+                        in_=x_sb[:, :, :, (D // Z_PASSES) * g : (D // Z_PASSES) * (g + 1)].rearrange("q f n d -> q n d f"),
+                    )
                 bias_ps = psum.tile([P, P], BF16, name="bias_ps", tag="bank")
                 nc.tensor.transpose(bias_ps[:], bias_rows[:], ident_bf[:])
                 nc.vector.tensor_copy(out=bias[:], in_=bias_ps[:, 0 : n_buf_rows + HID_CHUNKS])
                 for g in range(Z_PASSES):
-                    zt_ps = psum.tile([P, PACK, M], BF16, name="zt_ps", tag="bank")
-                    for t in range(PACK):
-                        for mt in range(M_TILES):
-                            nc.tensor.transpose(
-                                zt_ps[:, t, P * mt : P * (mt + 1)], x_perm[mt][:, g, t, :], ident_bf[:]
-                            )
+                    zt_ps = psum.tile([P, N_LO, P], BF16, name="zt_ps", tag="bank")
+                    for n in range(N_LO):
+                        nc.tensor.transpose(zt_ps[:, n, :], x_perm[:, n, g, :], ident_bf[:])
                     grouped = stage.tile([P, M, PACK], BF16, name="grouped_a", align_bytes=64)
-                    nc.scalar.copy(out=grouped[:], in_=zt_ps[:].rearrange("p t m -> p m t"))
+                    nc.scalar.copy(
+                        out=grouped[:].rearrange("p (n hb) t -> p n hb t", n=N_LO),
+                        in_=zt_ps[:].rearrange("p n (t hb) -> p n hb t", t=PACK),
+                    )
                     zt_grouped.append(grouped)
 
         zb_ps = []
@@ -274,8 +274,8 @@ def tile_interaction_net_pa_kernel(tc, z, cells, buf_W, buf_b, lam_W1, lam_b1, o
             if g == 1:
                 for c in range(HID_CHUNKS):
                     nc.scalar.activation(
-                        out=q_sb[:, c, :],
-                        in_=q_ps[c // 2][:, c % 2, :],
+                        out=q_sb[:, c, :].rearrange("p (b h n) -> p b h n", h=N_HI, n=N_LO),
+                        in_=q_ps[c // 2][:, c % 2, :].rearrange("p (n h b) -> p b h n", n=N_LO, h=N_HI),
                         func=ACT.Identity,
                         bias=bias[:, n_buf_rows + c : n_buf_rows + c + 1],
                         scale=1.0,

@@ -23,13 +23,16 @@ CELL_PASSES = CELL // K_PASS
 BUF_PASSES = BUF // K_PASS
 UNIT_COLS = 512
 HID_CHUNKS = HID // P
+HALVES = 2
+HALF_COLS = HID // HALVES
+HALF_CHUNKS = HID_CHUNKS // HALVES
 M_TILES = M // P
 N_HI = 2
 N_LO = N // N_HI
 F_HI = F // PACK
-GROUP_BATCHES = 2
-GROUP_ROWS = GROUP_BATCHES * N * N
-GROUP_TILES = GROUP_ROWS // P
+QUAD = 4
+QUADS = N // QUAD
+TILE_BATCHES = P // N
 
 FLOPS = 2 * M * (K_Z * BUF + CELL * HID + BUF * HID)
 
@@ -54,6 +57,13 @@ def tile_interaction_net_pa_kernel(tc, z, cells, buf_W, buf_b, lam_W1, lam_b1, o
 
         n_buf_rows = BUF // P
         x_sb = raws.tile([P, F_HI, N_LO, D], BF16)
+        for t in range(PACK):
+            for n_hi in range(N_HI):
+                part0 = B * (N_HI * t + n_hi)
+                nc.sync.dma_start(
+                    out=x_sb[part0 : part0 + B, :, :, :].rearrange("b f n d -> b f (n d)"),
+                    in_=z[:, t:F:PACK, N_LO * n_hi : N_LO * (n_hi + 1), :].rearrange("b f n d -> b f (n d)"),
+                )
         raw_units = []
         for cb in range(BUF_PASSES):
             for g in range(Z_PASSES):
@@ -65,14 +75,6 @@ def tile_interaction_net_pa_kernel(tc, z, cells, buf_W, buf_b, lam_W1, lam_b1, o
                     ),
                 )
                 raw_units.append(raw)
-            if cb == 0:
-                for t in range(PACK):
-                    for n_hi in range(N_HI):
-                        part0 = B * (N_HI * t + n_hi)
-                        nc.sync.dma_start(
-                            out=x_sb[part0 : part0 + B, :, :, :].rearrange("b f n d -> b f (n d)"),
-                            in_=z[:, t:F:PACK, N_LO * n_hi : N_LO * (n_hi + 1), :].rearrange("b f n d -> b f (n d)"),
-                        )
         cells_rows = cells.rearrange("b n k -> (b n) k")
         c_sb = []
         for mt in range(M_TILES):
@@ -109,22 +111,30 @@ def tile_interaction_net_pa_kernel(tc, z, cells, buf_W, buf_b, lam_W1, lam_b1, o
         for i in range(len(raw_units)):
             unit_codes.append(keep.tile([P, UNIT_COLS], U32, name="unit_codes%d" % i, align_bytes=64))
             unit_scales.append(keep.tile([P, UNIT_COLS], U8, name="unit_scales%d" % i, align_bytes=64))
+        grouped_units = {}
+        buf_unit = list(range(2 * BUF_PASSES))
+        low_unit = [len(buf_unit) + g for g in range(BUF_PASSES)]
+        top_unit = [len(buf_unit) + len(low_unit) + g for g in range(CELL_PASSES)]
 
-        def regroup_unit(i, on_scalar):
-            grouped = stage.tile([P, UNIT_COLS, PACK], BF16, name="grouped_w", align_bytes=64)
-            src = raw_units[i][:].rearrange("p t (c i) -> p c t i", i=4)
+        def regroup(unit, engine, half=None):
+            col0, width = (0, UNIT_COLS) if half is None else (HALF_COLS * half, HALF_COLS)
+            grouped = stage.tile(
+                [P, width, PACK], BF16, name="grouped_w%d" % width, bufs=6 if width < UNIT_COLS else 4, align_bytes=64
+            )
+            src = raw_units[unit][:, :, col0 : col0 + width].rearrange("p t (c i) -> p c t i", i=4)
             dst = grouped[:].rearrange("p (c i) t -> p c t i", i=4)
-            if on_scalar:
+            if engine == "scalar":
                 nc.scalar.copy(out=dst, in_=src)
             else:
                 nc.vector.tensor_copy(out=dst, in_=src)
-            return grouped
+            grouped_units[unit, half] = grouped
 
-        def quantise_unit(i, grouped):
+        def quantise(unit, half=None):
+            col0, width = (0, UNIT_COLS) if half is None else (HALF_COLS * half, HALF_COLS)
             nc.vector.quantize_mx(
-                out=unit_codes[i][:].bitcast(FP8X4),
-                scales=unit_scales[i][:],
-                in_=grouped[:].rearrange("p w t -> p (w t)"),
+                out=unit_codes[unit][:, col0 : col0 + width].bitcast(FP8X4),
+                scales=unit_scales[unit][:, col0 : col0 + width],
+                in_=grouped_units[unit, half][:].rearrange("p w t -> p (w t)"),
             )
 
         def quantise_rows(name, grouped_flat):
@@ -133,63 +143,58 @@ def tile_interaction_net_pa_kernel(tc, z, cells, buf_W, buf_b, lam_W1, lam_b1, o
             nc.vector.quantize_mx(out=codes[:].bitcast(FP8X4), scales=scales[:], in_=grouped_flat)
             return codes, scales
 
-        def mx_group(acc, weights, col0, rows):
-            n_pass = len(weights)
-            for g in range(n_pass):
-                nc.tensor.matmul_mx(
-                    out=acc,
-                    lhsT=unit_codes[weights[g]][:, col0 : col0 + P].bitcast(FP8X4),
-                    lhsT_scale=unit_scales[weights[g]][:, col0 : col0 + P],
-                    rhs=rows[g][0][:].bitcast(FP8X4),
-                    rhs_scale=rows[g][1][:],
-                    start=(g == 0),
-                    stop=(g == n_pass - 1),
-                )
+        def mx_pass(acc, unit, col0, row_codes, first, last):
+            nc.tensor.matmul_mx(
+                out=acc,
+                lhsT=unit_codes[unit][:, col0 : col0 + P].bitcast(FP8X4),
+                lhsT_scale=unit_scales[unit][:, col0 : col0 + P],
+                rhs=row_codes[0][:].bitcast(FP8X4),
+                rhs_scale=row_codes[1][:],
+                start=first,
+                stop=last,
+            )
 
+        def mx_group(acc, units, col0, rows):
+            for g in range(len(units)):
+                mx_pass(acc, units[g], col0, rows[g], g == 0, g == len(units) - 1)
+
+        x_perm = raws.tile([P, N_LO, Z_PASSES, P], BF16)
         zt_grouped = []
         zt_q = []
-        bias = const.tile([P, n_buf_rows + HID_CHUNKS], F32)
-        for pair in range(BUF_PASSES):
-            even = regroup_unit(2 * pair, False)
-            odd = regroup_unit(2 * pair + 1, pair > 0)
-            quantise_unit(2 * pair, even)
-            if pair == 1:
-                for g in range(Z_PASSES):
-                    zt_q.append(quantise_rows("zt%d" % g, zt_grouped[g][:].rearrange("p m t -> p (m t)")))
-            quantise_unit(2 * pair + 1, odd)
-            if pair == 0:
-                x_perm = raws.tile([P, N_LO, Z_PASSES, P], BF16)
-                for g in range(Z_PASSES):
-                    nc.vector.tensor_copy(
-                        out=x_perm[:, :, g, :].rearrange("q n (d f) -> q n d f", f=F_HI),
-                        in_=x_sb[:, :, :, (D // Z_PASSES) * g : (D // Z_PASSES) * (g + 1)].rearrange("q f n d -> q n d f"),
-                    )
-                bias_ps = psum.tile([P, P], BF16, name="bias_ps", tag="bank")
-                nc.tensor.transpose(bias_ps[:], bias_rows[:], ident_bf[:])
-                nc.vector.tensor_copy(out=bias[:], in_=bias_ps[:, 0 : n_buf_rows + HID_CHUNKS])
-                for g in range(Z_PASSES):
-                    zt_ps = psum.tile([P, N_LO, P], BF16, name="zt_ps", tag="bank")
-                    for n in range(N_LO):
-                        nc.tensor.transpose(zt_ps[:, n, :], x_perm[:, n, g, :], ident_bf[:])
-                    grouped = stage.tile([P, M, PACK], BF16, name="grouped_a", align_bytes=64)
-                    nc.scalar.copy(
-                        out=grouped[:].rearrange("p (n hb) t -> p n hb t", n=N_LO),
-                        in_=zt_ps[:].rearrange("p n (t hb) -> p n hb t", t=PACK),
-                    )
-                    zt_grouped.append(grouped)
+
+        def order_z(g):
+            nc.vector.tensor_copy(
+                out=x_perm[:, :, g, :].rearrange("q n (d f) -> q n d f", f=F_HI),
+                in_=x_sb[:, :, :, (D // Z_PASSES) * g : (D // Z_PASSES) * (g + 1)].rearrange("q f n d -> q n d f"),
+            )
+
+        def transpose_z(g):
+            zt_ps = psum.tile([P, N_LO, P], BF16, name="zt_ps", tag="bank")
+            for n in range(N_LO):
+                nc.tensor.transpose(zt_ps[:, n, :], x_perm[:, n, g, :], ident_bf[:])
+            grouped = stage.tile([P, M, PACK], BF16, name="grouped_a", align_bytes=64)
+            nc.scalar.copy(
+                out=grouped[:].rearrange("p (n hb) t -> p n hb t", n=N_LO),
+                in_=zt_ps[:].rearrange("p n (t hb) -> p n hb t", t=PACK),
+            )
+            zt_grouped.append(grouped)
+
+        def quantise_z(g):
+            zt_q.append(quantise_rows("zt%d" % g, zt_grouped[g][:].rearrange("p m t -> p (m t)")))
 
         zb_ps = []
         elu_parts = []
+        zb_grouped = []
         zb_q = []
 
         def buffer_passes(g2):
-            for half in range(2):
+            for pair in range(2):
                 acc = psum.tile([P, 2, M], F32, name="zb_ps", tag="bank")
                 for s in range(2):
-                    mx_group(acc[:, s, :], [2 * g2, 2 * g2 + 1], P * (2 * half + s), zt_q)
+                    mx_group(acc[:, s, :], [2 * g2, 2 * g2 + 1], P * (2 * pair + s), zt_q)
                 zb_ps.append(acc)
 
-        def bias_and_exp(g2):
+        def add_bias(g2):
             v_sb = stage.tile([P, PACK, M], F32, name="v_sb")
             for t in range(PACK):
                 nc.scalar.activation(
@@ -200,12 +205,18 @@ def tile_interaction_net_pa_kernel(tc, z, cells, buf_W, buf_b, lam_W1, lam_b1, o
                     scale=1.0,
                 )
             e_sb = stage.tile([P, PACK, M], F32, name="e_sb")
-            nc.scalar.activation(out=e_sb[:], in_=v_sb[:], func=ACT.Exp)
             elu_parts.append((v_sb, e_sb))
+
+        def exponential(g2):
+            v_sb, e_sb = elu_parts[g2]
+            nc.scalar.activation(out=e_sb[:], in_=v_sb[:], func=ACT.Exp)
+
+        def negative_part(g2):
+            e_sb = elu_parts[g2][1]
+            nc.vector.tensor_scalar(out=e_sb[:], in0=e_sb[:], scalar1=-1.0, scalar2=0.0, op0=ALU.add, op1=ALU.min)
 
         def finish_elu(g2):
             v_sb, e_sb = elu_parts[g2]
-            nc.vector.tensor_scalar(out=e_sb[:], in0=e_sb[:], scalar1=-1.0, scalar2=0.0, op0=ALU.add, op1=ALU.min)
             grouped = stage.tile([P, M, PACK], BF16, name="grouped_a", align_bytes=64)
             nc.vector.tensor_tensor(
                 out=grouped[:],
@@ -213,24 +224,16 @@ def tile_interaction_net_pa_kernel(tc, z, cells, buf_W, buf_b, lam_W1, lam_b1, o
                 in1=e_sb[:].rearrange("p t m -> p m t"),
                 op=ALU.max,
             )
-            return grouped
+            zb_grouped.append(grouped)
 
-        first_low = 2 * BUF_PASSES
-        low_grouped = []
-        buffer_passes(0)
-        for g2 in range(BUF_PASSES):
-            if g2 + 1 < BUF_PASSES:
-                buffer_passes(g2 + 1)
-            bias_and_exp(g2)
-            low_grouped.append(regroup_unit(first_low + g2, False))
-            if g2 > 0:
-                grouped = finish_elu(g2 - 1)
-                quantise_unit(first_low + g2 - 1, low_grouped[g2 - 1])
-                zb_q.append(quantise_rows("zb%d" % (g2 - 1), grouped[:].rearrange("p m t -> p (m t)")))
+        def quantise_zb(g2):
+            zb_q.append(quantise_rows("zb%d" % g2, zb_grouped[g2][:].rearrange("p m t -> p (m t)")))
 
-        first_top = first_low + BUF_PASSES
+        cells_ps = []
         cells_grouped = []
-        for g in range(CELL_PASSES):
+        cells_q = []
+
+        def transpose_cells(g):
             c_ps = psum.tile([P, 2, M], F32, name="c_ps", tag="bank")
             for u in range(2):
                 for mt in range(M_TILES):
@@ -238,73 +241,205 @@ def tile_interaction_net_pa_kernel(tc, z, cells, buf_W, buf_b, lam_W1, lam_b1, o
                     nc.tensor.transpose(
                         c_ps[:, u, P * mt : P * (mt + 1)], c_sb[mt][:].bitcast(F32)[:, word0 : word0 + P], ident_f32[:]
                     )
+            cells_ps.append(c_ps)
+
+        def group_cells(g):
             grouped = stage.tile([P, M * PACK], BF16, name="grouped_c", bufs=CELL_PASSES, align_bytes=64)
             nc.scalar.copy(
-                out=grouped[:].bitcast(F32).rearrange("p (m u) -> p m u", u=2), in_=c_ps[:].rearrange("p u m -> p m u")
+                out=grouped[:].bitcast(F32).rearrange("p (m u) -> p m u", u=2),
+                in_=cells_ps[g][:].rearrange("p u m -> p m u"),
             )
             cells_grouped.append(grouped)
-        top_grouped = [regroup_unit(first_top, True), regroup_unit(first_top + 1, True)]
-        grouped = finish_elu(BUF_PASSES - 1)
-        quantise_unit(first_top - 1, low_grouped[BUF_PASSES - 1])
-        zb_q.append(quantise_rows("zb%d" % (BUF_PASSES - 1), grouped[:].rearrange("p m t -> p (m t)")))
-        q_ps = []
-        for half in range(2):
-            acc = psum.tile([P, 2, M], F32, name="q_ps", tag="bank")
-            for s in range(2):
-                mx_group(acc[:, s, :], [first_low + g for g in range(BUF_PASSES)], P * (2 * half + s), zb_q)
-            q_ps.append(acc)
-        cells_q = [quantise_rows("cells%d" % g, cells_grouped[g][:]) for g in range(CELL_PASSES)]
 
-        p_ps = [psum_p.tile([P, M], F32, name="p_ps%d" % c) for c in range(HID_CHUNKS)]
+        def quantise_cells(g):
+            cells_q.append(quantise_rows("cells%d" % g, cells_grouped[g][:]))
+
         q_sb = keep.tile([P, HID_CHUNKS, M], F32)
-        for g in range(CELL_PASSES):
-            if g + 2 < CELL_PASSES:
-                top_grouped.append(regroup_unit(first_top + g + 2, g + 3 < CELL_PASSES))
-            quantise_unit(first_top + g, top_grouped[g])
-            for c in range(HID_CHUNKS):
-                nc.tensor.matmul_mx(
-                    out=p_ps[c][:],
-                    lhsT=unit_codes[first_top + g][:, P * c : P * (c + 1)].bitcast(FP8X4),
-                    lhsT_scale=unit_scales[first_top + g][:, P * c : P * (c + 1)],
-                    rhs=cells_q[g][0][:].bitcast(FP8X4),
-                    rhs_scale=cells_q[g][1][:],
-                    start=(g == 0),
-                    stop=(g == CELL_PASSES - 1),
-                )
-            if g == 1:
-                for c in range(HID_CHUNKS):
-                    nc.scalar.activation(
-                        out=q_sb[:, c, :].rearrange("p (b h n) -> p b h n", h=N_HI, n=N_LO),
-                        in_=q_ps[c // 2][:, c % 2, :].rearrange("p (n h b) -> p b h n", n=N_LO, h=N_HI),
-                        func=ACT.Identity,
-                        bias=bias[:, n_buf_rows + c : n_buf_rows + c + 1],
-                        scale=1.0,
-                    )
-                nc.scalar.activation(out=warm[:, 3:4], in_=warm[:, 2:3], func=ACT.Gelu)
+        p_ps = [psum_p.tile([P, M], F32, name="p_ps%d" % c) for c in range(HID_CHUNKS)]
+        q_ps = {}
 
-        out_rows = out.rearrange("b i j h -> (b i j) h")
-        for grp in range(B // GROUP_BATCHES):
-            m0 = GROUP_BATCHES * N * grp
-            m1 = m0 + GROUP_BATCHES * N
-            sums = stage.tile([P, HID_CHUNKS, GROUP_ROWS], F32, name="sums")
-            for c in range(HID_CHUNKS):
-                nc.vector.tensor_tensor(
-                    out=sums[:, c, :].rearrange("p (b i j) -> p b i j", i=N, j=N),
-                    in0=p_ps[c][:, m0:m1]
-                    .rearrange("p (b i) -> p b i", i=N)
-                    .unsqueeze(3)
-                    .to_broadcast([P, GROUP_BATCHES, N, N]),
-                    in1=q_sb[:, c, m0:m1]
-                    .rearrange("p (b j) -> p b j", j=N)
-                    .unsqueeze(2)
-                    .to_broadcast([P, GROUP_BATCHES, N, N]),
-                    op=ALU.add,
+        def q_passes(half):
+            acc = psum.tile([P, HALF_CHUNKS, M], F32, name="q_ps", tag="bank")
+            for s in range(HALF_CHUNKS):
+                mx_group(acc[:, s, :], low_unit, HALF_COLS * half + P * s, zb_q)
+            q_ps[half] = acc
+
+        def move_q(half):
+            for s in range(HALF_CHUNKS):
+                c = HALF_CHUNKS * half + s
+                nc.scalar.activation(
+                    out=q_sb[:, c, :].rearrange("p (b h n) -> p b h n", h=N_HI, n=N_LO),
+                    in_=q_ps[half][:, s, :].rearrange("p (n h b) -> p b h n", n=N_LO, h=N_HI),
+                    func=ACT.Identity,
+                    bias=bias[:, n_buf_rows + c : n_buf_rows + c + 1],
+                    scale=1.0,
                 )
-            for r in range(GROUP_TILES):
-                o_ps = psum.tile([P, HID], F32, name="o_ps", tag="bank")
-                for c in range(HID_CHUNKS):
-                    nc.tensor.transpose(o_ps[:, P * c : P * (c + 1)], sums[:, c, P * r : P * (r + 1)], ident_f32[:])
-                o_sb = stage.tile([P, HID], F32, name="o_sb", bufs=10)
-                nc.scalar.activation(out=o_sb[:], in_=o_ps[:], func=ACT.Gelu)
-                row0 = GROUP_ROWS * grp + P * r
-                nc.sync.dma_start(out=out_rows[row0 : row0 + P, :], in_=o_sb[:])
+
+        def p_passes(half, g):
+            for c in range(HALF_CHUNKS * half, HALF_CHUNKS * (half + 1)):
+                mx_pass(p_ps[c][:], top_unit[g], P * c, cells_q[g], g == 0, g == CELL_PASSES - 1)
+
+        bias = const.tile([P, n_buf_rows + HID_CHUNKS], F32)
+        order_z(0)
+        order_z(1)
+        transpose_z(0)
+        transpose_z(1)
+        bias_ps = psum.tile([P, P], BF16, name="bias_ps", tag="bank")
+        nc.tensor.transpose(bias_ps[:], bias_rows[:], ident_bf[:])
+        regroup(0, "vector")
+        nc.vector.tensor_copy(out=bias[:], in_=bias_ps[:, 0 : n_buf_rows + HID_CHUNKS])
+        regroup(1, "vector")
+        regroup(2, "scalar")
+        regroup(3, "scalar")
+        quantise_z(0)
+        quantise(0)
+        quantise_z(1)
+        quantise(1)
+        buffer_passes(0)
+        add_bias(0)
+        exponential(0)
+        regroup(4, "vector")
+        quantise(2)
+        regroup(5, "vector")
+        quantise(3)
+        buffer_passes(1)
+        add_bias(1)
+        quantise(4)
+        quantise(5)
+        transpose_cells(0)
+        transpose_cells(1)
+        buffer_passes(2)
+        transpose_cells(2)
+        transpose_cells(3)
+        group_cells(0)
+        exponential(1)
+        group_cells(1)
+        add_bias(2)
+        exponential(2)
+        group_cells(2)
+        group_cells(3)
+        regroup(top_unit[0], "scalar", 0)
+        regroup(top_unit[2], "scalar", 0)
+        regroup(top_unit[3], "scalar", 0)
+        nc.scalar.activation(out=warm[:, 3:4], in_=warm[:, 2:3], func=ACT.Gelu)
+
+        negative_part(0)
+        regroup(low_unit[0], "vector", 0)
+        finish_elu(0)
+        regroup(low_unit[1], "vector", 0)
+        quantise_zb(0)
+        quantise(low_unit[0], 0)
+        quantise(low_unit[1], 0)
+        negative_part(1)
+        quantise_cells(0)
+        finish_elu(1)
+        quantise_cells(1)
+        regroup(low_unit[2], "vector", 0)
+        quantise_zb(1)
+        negative_part(2)
+        quantise(low_unit[2], 0)
+        finish_elu(2)
+        regroup(top_unit[1], "vector", 0)
+        quantise_zb(2)
+        q_passes(0)
+        move_q(0)
+        quantise_cells(2)
+        quantise_cells(3)
+        for g in range(CELL_PASSES - 1):
+            quantise(top_unit[g], 0)
+            p_passes(0, g)
+        regroup(low_unit[0], "vector", 1)
+        quantise(top_unit[3], 0)
+        p_passes(0, 3)
+        p_sb = keep.tile([P, HALF_CHUNKS, M], F32)
+        nc.scalar.copy(out=p_sb[:, 0, :], in_=p_ps[0][:])
+
+        out_slots = out.rearrange("b i j h -> (b i) j h")
+
+        def q_of_slots(c, mt, quad):
+            return (
+                q_sb[:, c, P * mt : P * (mt + 1)]
+                .rearrange("p (b j) -> p j b", j=N)[:, QUAD * quad : QUAD * (quad + 1), :]
+                .unsqueeze(3)
+                .to_broadcast([P, QUAD, TILE_BATCHES, N])
+            )
+
+        def sum_on_vector(c, mt, quad):
+            sums = stage.tile([P, QUAD, P], F32, name="sums", bufs=8)
+            nc.vector.tensor_tensor(
+                out=sums[:].rearrange("p j (b i) -> p j b i", i=N),
+                in0=p_ps[c][:, P * mt : P * (mt + 1)]
+                .rearrange("p (b i) -> p b i", i=N)
+                .unsqueeze(1)
+                .to_broadcast([P, QUAD, TILE_BATCHES, N]),
+                in1=q_of_slots(c, mt, quad),
+                op=ALU.add,
+            )
+            return [sums]
+
+        def sum_on_tensor(c, mt, quad):
+            rep = stage.tile([P, QUAD, P], F32, name="rep", bufs=4)
+            nc.vector.tensor_copy(out=rep[:].rearrange("p j (b i) -> p j b i", i=N), in_=q_of_slots(c, mt, quad))
+            return [p_sb[:, c, P * mt : P * (mt + 1)], rep]
+
+        def output_group(half, mt, quad):
+            sources = []
+            for s in range(HALF_CHUNKS):
+                c = HALF_CHUNKS * half + s
+                if c == 0:
+                    sources.append(sum_on_tensor(c, mt, quad))
+                else:
+                    sources.append(sum_on_vector(c, mt, quad))
+            o_sb = stage.tile([P, QUAD, HALF_COLS], F32, name="o_sb", bufs=6)
+            for pair in range(QUAD // 2):
+                o_ps = psum.tile([P, 2, HALF_COLS], F32, name="o_ps", tag="bank")
+                for e in range(2):
+                    j = 2 * pair + e
+                    for s in range(HALF_CHUNKS):
+                        parts = sources[s]
+                        for n, part in enumerate(parts):
+                            nc.tensor.matmul(
+                                o_ps[:, e, P * s : P * (s + 1)],
+                                lhsT=part[:, j, :] if n == len(parts) - 1 else part,
+                                rhs=ident_f32[:],
+                                start=(n == 0),
+                                stop=(n == len(parts) - 1),
+                                is_transpose=True,
+                            )
+                nc.scalar.activation(out=o_sb[:, 2 * pair : 2 * pair + 2, :], in_=o_ps[:], func=ACT.Gelu)
+            nc.sync.dma_start(
+                out=out_slots[
+                    P * mt : P * (mt + 1), QUAD * quad : QUAD * (quad + 1), HALF_COLS * half : HALF_COLS * (half + 1)
+                ],
+                in_=o_sb[:],
+            )
+
+        for grp in range(M_TILES * QUADS):
+            output_group(0, grp // QUADS, grp % QUADS)
+            if grp == 1:
+                regroup(low_unit[1], "vector", 1)
+                regroup(low_unit[2], "vector", 1)
+                quantise(low_unit[0], 1)
+            elif grp == 2:
+                quantise(low_unit[1], 1)
+                quantise(low_unit[2], 1)
+                q_passes(1)
+            elif grp == 3:
+                move_q(1)
+                regroup(top_unit[0], "vector", 1)
+                regroup(top_unit[1], "vector", 1)
+            elif grp == 4:
+                quantise(top_unit[0], 1)
+                regroup(top_unit[2], "vector", 1)
+                quantise(top_unit[1], 1)
+            elif grp == 5:
+                p_passes(1, 0)
+                p_passes(1, 1)
+                regroup(top_unit[3], "vector", 1)
+                quantise(top_unit[2], 1)
+            elif grp == 6:
+                quantise(top_unit[3], 1)
+                p_passes(1, 2)
+                p_passes(1, 3)
+        for grp in range(M_TILES * QUADS):
+            output_group(1, grp // QUADS, grp % QUADS)

@@ -64,6 +64,7 @@ def tile_interaction_net_pa_kernel(tc, z, cells, buf_W, buf_b, lam_W1, lam_b1, o
                     out=x_sb[part0 : part0 + B, :, :, :].rearrange("b f n d -> b f (n d)"),
                     in_=z[:, t:F:PACK, N_LO * n_hi : N_LO * (n_hi + 1), :].rearrange("b f n d -> b f (n d)"),
                 )
+        nc.scalar.activation(out=warm[:, 1:2], in_=warm[:, 0:1], func=ACT.Exp)
         raw_units = []
         for cb in range(BUF_PASSES):
             for g in range(Z_PASSES):
@@ -75,6 +76,11 @@ def tile_interaction_net_pa_kernel(tc, z, cells, buf_W, buf_b, lam_W1, lam_b1, o
                     ),
                 )
                 raw_units.append(raw)
+            if cb == 0:
+                nc.sync.dma_start(out=bias_rows[0:n_buf_rows, :], in_=buf_b.rearrange("(r c) -> r c", c=P))
+                nc.sync.dma_start(
+                    out=bias_rows[n_buf_rows : n_buf_rows + HID_CHUNKS, :], in_=lam_b1.rearrange("(r c) -> r c", c=P)
+                )
         cells_rows = cells.rearrange("b n k -> (b n) k")
         c_sb = []
         for mt in range(M_TILES):
@@ -98,13 +104,8 @@ def tile_interaction_net_pa_kernel(tc, z, cells, buf_W, buf_b, lam_W1, lam_b1, o
                 )
             raw_units.append(raw)
 
-        nc.scalar.activation(out=warm[:, 1:2], in_=warm[:, 0:1], func=ACT.Exp)
         make_identity(nc, ident_bf[:])
         make_identity(nc, ident_f32[:])
-        nc.gpsimd.dma_start(out=bias_rows[0:n_buf_rows, :], in_=buf_b.rearrange("(r c) -> r c", c=P))
-        nc.gpsimd.dma_start(
-            out=bias_rows[n_buf_rows : n_buf_rows + HID_CHUNKS, :], in_=lam_b1.rearrange("(r c) -> r c", c=P)
-        )
 
         unit_codes = []
         unit_scales = []
@@ -287,7 +288,6 @@ def tile_interaction_net_pa_kernel(tc, z, cells, buf_W, buf_b, lam_W1, lam_b1, o
         bias_ps = psum.tile([P, P], BF16, name="bias_ps", tag="bank")
         nc.tensor.transpose(bias_ps[:], bias_rows[:], ident_bf[:])
         regroup(0, "vector")
-        nc.vector.tensor_copy(out=bias[:], in_=bias_ps[:, 0 : n_buf_rows + HID_CHUNKS])
         regroup(1, "vector")
         regroup(2, "scalar")
         regroup(3, "scalar")
@@ -295,6 +295,7 @@ def tile_interaction_net_pa_kernel(tc, z, cells, buf_W, buf_b, lam_W1, lam_b1, o
         quantise(0)
         quantise_z(1)
         quantise(1)
+        nc.vector.tensor_copy(out=bias[:], in_=bias_ps[:, 0 : n_buf_rows + HID_CHUNKS])
         buffer_passes(0)
         add_bias(0)
         exponential(0)

@@ -352,8 +352,12 @@ def tile_interaction_net_pa_kernel(tc, z, cells, buf_W, buf_b, lam_W1, lam_b1, o
         regroup(low_unit[0], "vector", 1)
         quantise(top_unit[3], 0)
         p_passes(0, 3)
-        p_sb = keep.tile([P, HALF_CHUNKS, M], F32)
-        nc.scalar.copy(out=p_sb[:, 0, :], in_=p_ps[0][:])
+        p_sb = [keep.tile([P, M], F32, name="p_sb%d" % half) for half in range(HALVES)]
+
+        def copy_p(half):
+            nc.scalar.copy(out=p_sb[half][:], in_=p_ps[HALF_CHUNKS * half][:])
+
+        copy_p(0)
 
         out_slots = out.rearrange("b i j h -> (b i) j h")
 
@@ -381,16 +385,21 @@ def tile_interaction_net_pa_kernel(tc, z, cells, buf_W, buf_b, lam_W1, lam_b1, o
         def sum_on_tensor(c, mt, quad):
             rep = stage.tile([P, QUAD, P], F32, name="rep", bufs=4)
             nc.vector.tensor_copy(out=rep[:].rearrange("p j (b i) -> p j b i", i=N), in_=q_of_slots(c, mt, quad))
-            return [p_sb[:, c, P * mt : P * (mt + 1)], rep]
+            return [p_sb[c // HALF_CHUNKS][:, P * mt : P * (mt + 1)], rep]
 
-        def output_group(half, mt, quad):
+        def group_sums(half, grp, first_on_tensor):
+            mt, quad = divmod(grp, QUADS)
             sources = []
             for s in range(HALF_CHUNKS):
                 c = HALF_CHUNKS * half + s
-                if c == 0:
+                if s == 0 and first_on_tensor:
                     sources.append(sum_on_tensor(c, mt, quad))
                 else:
                     sources.append(sum_on_vector(c, mt, quad))
+            return sources
+
+        def finish_group(half, grp, sources):
+            mt, quad = divmod(grp, QUADS)
             o_sb = stage.tile([P, QUAD, HALF_COLS], F32, name="o_sb", bufs=6)
             for pair in range(QUAD // 2):
                 o_ps = psum.tile([P, 2, HALF_COLS], F32, name="o_ps", tag="bank")
@@ -415,9 +424,16 @@ def tile_interaction_net_pa_kernel(tc, z, cells, buf_W, buf_b, lam_W1, lam_b1, o
                 in_=o_sb[:],
             )
 
+        def keep_busy():
+            busy_ps = psum_p.tile([P, UNIT_COLS], F32, name="busy_ps", tag="p_ps0")
+            nc.tensor.matmul(busy_ps[:], lhsT=ident_bf[:], rhs=raw_units[0][:, 0, :], start=True, stop=True)
+
         for grp in range(M_TILES * QUADS):
-            output_group(0, grp // QUADS, grp % QUADS)
+            finish_group(0, grp, group_sums(0, grp, True))
+            if grp not in (2, 5, 6):
+                keep_busy()
             if grp == 1:
+                regroup(top_unit[2], "scalar", 1)
                 regroup(low_unit[1], "vector", 1)
                 regroup(low_unit[2], "vector", 1)
                 quantise(low_unit[0], 1)
@@ -431,7 +447,6 @@ def tile_interaction_net_pa_kernel(tc, z, cells, buf_W, buf_b, lam_W1, lam_b1, o
                 regroup(top_unit[1], "vector", 1)
             elif grp == 4:
                 quantise(top_unit[0], 1)
-                regroup(top_unit[2], "vector", 1)
                 quantise(top_unit[1], 1)
             elif grp == 5:
                 p_passes(1, 0)
@@ -443,4 +458,9 @@ def tile_interaction_net_pa_kernel(tc, z, cells, buf_W, buf_b, lam_W1, lam_b1, o
                 p_passes(1, 2)
                 p_passes(1, 3)
         for grp in range(M_TILES * QUADS):
-            output_group(1, grp // QUADS, grp % QUADS)
+            sources = group_sums(1, grp, grp % 2 == 1)
+            if grp == 0:
+                copy_p(1)
+            finish_group(1, grp, sources)
+            if grp in (1, 3, 5):
+                keep_busy()

@@ -57,11 +57,10 @@ def tile_interaction_net_pa_kernel(tc, z, cells, buf_W, buf_b, lam_W1, lam_b1, o
 
         n_buf_rows = BUF // P
         x_sb = raws.tile([P, F_HI, N_LO, D], BF16)
-        for t in range(PACK):
-            for n_hi in range(N_HI):
-                part0 = B * (N_HI * t + n_hi)
+        for n_hi in range(N_HI):
+            for t in (0, 2, 1, 3):
                 nc.sync.dma_start(
-                    out=x_sb[part0 : part0 + B, :, :, :].rearrange("b f n d -> b f (n d)"),
+                    out=x_sb[N_HI * t + n_hi : P : N_HI * PACK, :, :, :].rearrange("b f n d -> b f (n d)"),
                     in_=z[:, t:F:PACK, N_LO * n_hi : N_LO * (n_hi + 1), :].rearrange("b f n d -> b f (n d)"),
                 )
         nc.scalar.activation(out=warm[:, 1:2], in_=warm[:, 0:1], func=ACT.Exp)
@@ -77,7 +76,10 @@ def tile_interaction_net_pa_kernel(tc, z, cells, buf_W, buf_b, lam_W1, lam_b1, o
                 )
                 raw_units.append(raw)
             if cb == 0:
-                nc.sync.dma_start(out=bias_rows[0:n_buf_rows, :], in_=buf_b.rearrange("(r c) -> r c", c=P))
+                for r0, r1 in ((0, 8), (8, n_buf_rows)):
+                    nc.sync.dma_start(
+                        out=bias_rows[r0:r1, :], in_=buf_b[P * r0 : P * r1].rearrange("(r c) -> r c", c=P)
+                    )
                 nc.sync.dma_start(
                     out=bias_rows[n_buf_rows : n_buf_rows + HID_CHUNKS, :], in_=lam_b1.rearrange("(r c) -> r c", c=P)
                 )
@@ -175,8 +177,8 @@ def tile_interaction_net_pa_kernel(tc, z, cells, buf_W, buf_b, lam_W1, lam_b1, o
                 nc.tensor.transpose(zt_ps[:, n, :], x_perm[:, n, g, :], ident_bf[:])
             grouped = stage.tile([P, M, PACK], BF16, name="grouped_a", align_bytes=64)
             nc.scalar.copy(
-                out=grouped[:].rearrange("p (n hb) t -> p n hb t", n=N_LO),
-                in_=zt_ps[:].rearrange("p n (t hb) -> p n hb t", t=PACK),
+                out=grouped[:].rearrange("p (nb h) t -> p nb h t", h=N_HI),
+                in_=zt_ps[:].rearrange("p n (b t h) -> p (n b) h t", t=PACK, h=N_HI),
             )
             zt_grouped.append(grouped)
 
@@ -270,7 +272,7 @@ def tile_interaction_net_pa_kernel(tc, z, cells, buf_W, buf_b, lam_W1, lam_b1, o
                 c = HALF_CHUNKS * half + s
                 nc.scalar.activation(
                     out=q_sb[:, c, :].rearrange("p (b h n) -> p b h n", h=N_HI, n=N_LO),
-                    in_=q_ps[half][:, s, :].rearrange("p (n h b) -> p b h n", n=N_LO, h=N_HI),
+                    in_=q_ps[half][:, s, :].rearrange("p (n b h) -> p b h n", n=N_LO, h=N_HI),
                     func=ACT.Identity,
                     bias=bias[:, n_buf_rows + c : n_buf_rows + c + 1],
                     scale=1.0,

from contextlib import ExitStack

import concourse.mybir as mybir
from concourse.masks import make_identity

BF16 = mybir.dt.bfloat16
F32 = mybir.dt.float32
U32 = mybir.dt.uint32
U8 = mybir.dt.uint8
FP8X4 = mybir.dt.float8_e4m3fn_x4
ACT = mybir.ActivationFunctionType
ALU = mybir.AluOpType

P = 128
PACK = 4
K_PASS = P * PACK

B, F, N, D, HID, CELL, BUF = 16, 16, 16, 64, 512, 2048, 1536
M = B * N
K_Z = D * F
Z_PASSES = K_Z // K_PASS
CELL_PASSES = CELL // K_PASS
BUF_PASSES = BUF // K_PASS
UNIT_COLS = 512
HID_CHUNKS = HID // P
HALVES = 2
HALF_COLS = HID // HALVES
HALF_CHUNKS = HID_CHUNKS // HALVES
M_TILES = M // P
N_HI = 2
N_LO = N // N_HI
F_HI = F // PACK
QUAD = 4
QUADS = N // QUAD
TILE_BATCHES = P // N

FLOPS = 2 * M * (K_Z * BUF + CELL * HID + BUF * HID)


def tile_interaction_net_pa_kernel(tc, z, cells, buf_W, buf_b, lam_W1, lam_b1, out):
    nc = tc.nc
    with ExitStack() as stack:
        const = stack.enter_context(tc.tile_pool(name="const", bufs=1))
        raws = stack.enter_context(tc.tile_pool(name="raws", bufs=1))
        keep = stack.enter_context(tc.tile_pool(name="keep", bufs=1))
        stage = stack.enter_context(tc.tile_pool(name="stage", bufs=3))
        psum = stack.enter_context(tc.psum_pool(name="psum", bufs=4))
        psum_p = stack.enter_context(tc.psum_pool(name="psum_p", bufs=1))
        stack.enter_context(tc.manual_schedule())

        ident_bf = const.tile([P, P], BF16)
        ident_f32 = const.tile([P, P], F32)
        bias_rows = const.tile([P, P], BF16)
        nc.vector.memset(bias_rows[:], 0.0)
        warm = const.tile([P, 4], F32)
        nc.vector.memset(warm[:], 0.0)

        n_buf_rows = BUF // P
        x_sb = raws.tile([P, F_HI, N_LO, D], BF16)
        for n_hi in range(N_HI):
            for t in (0, 2, 1, 3):
                nc.sync.dma_start(
                    out=x_sb[N_HI * t + n_hi : P : N_HI * PACK, :, :, :].rearrange("b f n d -> b f (n d)"),
                    in_=z[:, t:F:PACK, N_LO * n_hi : N_LO * (n_hi + 1), :].rearrange("b f n d -> b f (n d)"),
                )
        nc.scalar.activation(out=warm[:, 1:2], in_=warm[:, 0:1], func=ACT.Exp)
        raw_units = []
        for cb in range(BUF_PASSES):
            for g in range(Z_PASSES):
                raw = raws.tile([P, PACK, UNIT_COLS], BF16, name="raw_buf%d_%d" % (cb, g))
                nc.sync.dma_start(
                    out=raw[:],
                    in_=buf_W[K_PASS * g : K_PASS * (g + 1), UNIT_COLS * cb : UNIT_COLS * (cb + 1)].rearrange(
                        "(p t) w -> p t w", t=PACK
                    ),
                )
                raw_units.append(raw)
            if cb == 0:
                for r0, r1 in ((0, 8), (8, n_buf_rows)):
                    nc.sync.dma_start(
                        out=bias_rows[r0:r1, :], in_=buf_b[P * r0 : P * r1].rearrange("(r c) -> r c", c=P)
                    )
                nc.sync.dma_start(
                    out=bias_rows[n_buf_rows : n_buf_rows + HID_CHUNKS, :], in_=lam_b1.rearrange("(r c) -> r c", c=P)
                )
        cells_rows = cells.rearrange("b n k -> (b n) k")
        c_sb = []
        for mt in range(M_TILES):
            c_tile = raws.tile([P, CELL], BF16, name="c_sb%d" % mt)
            nc.sync.dma_start(out=c_tile[:], in_=cells_rows[P * mt : P * (mt + 1), :])
            c_sb.append(c_tile)
        for g in range(BUF_PASSES):
            raw = raws.tile([P, PACK, UNIT_COLS], BF16, name="raw_bot%d" % g)
            nc.sync.dma_start(
                out=raw[:],
                in_=lam_W1[CELL + K_PASS * g : CELL + K_PASS * (g + 1), :].rearrange("(t p) w -> p t w", p=P),
            )
            raw_units.append(raw)
        for g in range(CELL_PASSES):
            raw = raws.tile([P, PACK, UNIT_COLS], BF16, name="raw_top%d" % g)
            for u in range(2):
                row0 = K_PASS * g + 2 * P * u
                nc.sync.dma_start(
                    out=raw[:, 2 * u : 2 * u + 2, :],
                    in_=lam_W1[row0 : row0 + 2 * P, :].rearrange("(p e) w -> p e w", e=2),
                )
            raw_units.append(raw)

        make_identity(nc, ident_bf[:])
        make_identity(nc, ident_f32[:])

        unit_codes = []
        unit_scales = []
        for i in range(len(raw_units)):
            unit_codes.append(keep.tile([P, UNIT_COLS], U32, name="unit_codes%d" % i, align_bytes=64))
            unit_scales.append(keep.tile([P, UNIT_COLS], U8, name="unit_scales%d" % i, align_bytes=64))
        grouped_units = {}
        buf_unit = list(range(2 * BUF_PASSES))
        low_unit = [len(buf_unit) + g for g in range(BUF_PASSES)]
        top_unit = [len(buf_unit) + len(low_unit) + g for g in range(CELL_PASSES)]

        def regroup(unit, engine, half=None):
            col0, width = (0, UNIT_COLS) if half is None else (HALF_COLS * half, HALF_COLS)
            grouped = stage.tile(
                [P, width, PACK], BF16, name="grouped_w%d" % width, bufs=6 if width < UNIT_COLS else 4, align_bytes=64
            )
            src = raw_units[unit][:, :, col0 : col0 + width].rearrange("p t (c i) -> p c t i", i=4)
            dst = grouped[:].rearrange("p (c i) t -> p c t i", i=4)
            if engine == "scalar":
                nc.scalar.copy(out=dst, in_=src)
            else:
                nc.vector.tensor_copy(out=dst, in_=src)
            grouped_units[unit, half] = grouped

        def quantise(unit, half=None):
            col0, width = (0, UNIT_COLS) if half is None else (HALF_COLS * half, HALF_COLS)
            nc.vector.quantize_mx(
                out=unit_codes[unit][:, col0 : col0 + width].bitcast(FP8X4),
                scales=unit_scales[unit][:, col0 : col0 + width],
                in_=grouped_units[unit, half][:].rearrange("p w t -> p (w t)"),
            )

        def quantise_rows(name, grouped_flat):
            codes = keep.tile([P, M], U32, name=name + "_codes", align_bytes=64)
            scales = keep.tile([P, M], U8, name=name + "_scales", align_bytes=64)
            nc.vector.quantize_mx(out=codes[:].bitcast(FP8X4), scales=scales[:], in_=grouped_flat)
            return codes, scales

        def mx_pass(acc, unit, col0, row_codes, first, last):
            nc.tensor.matmul_mx(
                out=acc,
                lhsT=unit_codes[unit][:, col0 : col0 + P].bitcast(FP8X4),
                lhsT_scale=unit_scales[unit][:, col0 : col0 + P],
                rhs=row_codes[0][:].bitcast(FP8X4),
                rhs_scale=row_codes[1][:],
                start=first,
                stop=last,
            )

        def mx_group(acc, units, col0, rows):
            for g in range(len(units)):
                mx_pass(acc, units[g], col0, rows[g], g == 0, g == len(units) - 1)

        x_perm = raws.tile([P, N_LO, Z_PASSES, P], BF16)
        zt_grouped = []
        zt_q = []

        def order_z(g):
            nc.vector.tensor_copy(
                out=x_perm[:, :, g, :].rearrange("q n (d f) -> q n d f", f=F_HI),
                in_=x_sb[:, :, :, (D // Z_PASSES) * g : (D // Z_PASSES) * (g + 1)].rearrange("q f n d -> q n d f"),
            )

        def transpose_z(g):
            zt_ps = psum.tile([P, N_LO, P], BF16, name="zt_ps", tag="bank")
            for n in range(N_LO):
                nc.tensor.transpose(zt_ps[:, n, :], x_perm[:, n, g, :], ident_bf[:])
            grouped = stage.tile([P, M, PACK], BF16, name="grouped_a", align_bytes=64)
            nc.scalar.copy(
                out=grouped[:].rearrange("p (nb h) t -> p nb h t", h=N_HI),
                in_=zt_ps[:].rearrange("p n (b t h) -> p (n b) h t", t=PACK, h=N_HI),
            )
            zt_grouped.append(grouped)

        def quantise_z(g):
            zt_q.append(quantise_rows("zt%d" % g, zt_grouped[g][:].rearrange("p m t -> p (m t)")))

        zb_ps = []
        elu_parts = []
        zb_grouped = []
        zb_q = []

        def buffer_passes(g2):
            for pair in range(2):
                acc = psum.tile([P, 2, M], F32, name="zb_ps", tag="bank")
                for s in range(2):
                    mx_group(acc[:, s, :], [2 * g2, 2 * g2 + 1], P * (2 * pair + s), zt_q)
                zb_ps.append(acc)

        def add_bias(g2):
            v_sb = stage.tile([P, PACK, M], F32, name="v_sb")
            for t in range(PACK):
                nc.scalar.activation(
                    out=v_sb[:, t, :],
                    in_=zb_ps[2 * g2 + t // 2][:, t % 2, :],
                    func=ACT.Identity,
                    bias=bias[:, PACK * g2 + t : PACK * g2 + t + 1],
                    scale=1.0,
                )
            e_sb = stage.tile([P, PACK, M], F32, name="e_sb")
            elu_parts.append((v_sb, e_sb))

        def exponential(g2):
            v_sb, e_sb = elu_parts[g2]
            nc.scalar.activation(out=e_sb[:], in_=v_sb[:], func=ACT.Exp)

        def negative_part(g2):
            e_sb = elu_parts[g2][1]
            nc.vector.tensor_scalar(out=e_sb[:], in0=e_sb[:], scalar1=-1.0, scalar2=0.0, op0=ALU.add, op1=ALU.min)

        def finish_elu(g2):
            v_sb, e_sb = elu_parts[g2]
            grouped = stage.tile([P, M, PACK], BF16, name="grouped_a", align_bytes=64)
            nc.vector.tensor_tensor(
                out=grouped[:],
                in0=v_sb[:].rearrange("p t m -> p m t"),
                in1=e_sb[:].rearrange("p t m -> p m t"),
                op=ALU.max,
            )
            zb_grouped.append(grouped)

        def quantise_zb(g2):
            zb_q.append(quantise_rows("zb%d" % g2, zb_grouped[g2][:].rearrange("p m t -> p (m t)")))

        cells_ps = []
        cells_grouped = []
        cells_q = []

        def transpose_cells(g):
            c_ps = psum.tile([P, 2, M], F32, name="c_ps", tag="bank")
            for u in range(2):
                for mt in range(M_TILES):
                    word0 = (K_PASS // 2) * g + P * u
                    nc.tensor.transpose(
                        c_ps[:, u, P * mt : P * (mt + 1)], c_sb[mt][:].bitcast(F32)[:, word0 : word0 + P], ident_f32[:]
                    )
            cells_ps.append(c_ps)

        def group_cells(g):
            grouped = stage.tile([P, M * PACK], BF16, name="grouped_c", bufs=CELL_PASSES, align_bytes=64)
            nc.scalar.copy(
                out=grouped[:].bitcast(F32).rearrange("p (m u) -> p m u", u=2),
                in_=cells_ps[g][:].rearrange("p u m -> p m u"),
            )
            cells_grouped.append(grouped)

        def quantise_cells(g):
            cells_q.append(quantise_rows("cells%d" % g, cells_grouped[g][:]))

        q_sb = keep.tile([P, HID_CHUNKS, M], F32)
        p_ps = [psum_p.tile([P, M], F32, name="p_ps%d" % c) for c in range(HID_CHUNKS)]
        q_ps = {}

        def q_passes(half):
            acc = psum.tile([P, HALF_CHUNKS, M], F32, name="q_ps", tag="bank")
            for s in range(HALF_CHUNKS):
                mx_group(acc[:, s, :], low_unit, HALF_COLS * half + P * s, zb_q)
            q_ps[half] = acc

        def move_q(half):
            for s in range(HALF_CHUNKS):
                c = HALF_CHUNKS * half + s
                nc.scalar.activation(
                    out=q_sb[:, c, :].rearrange("p (b h n) -> p b h n", h=N_HI, n=N_LO),
                    in_=q_ps[half][:, s, :].rearrange("p (n b h) -> p b h n", n=N_LO, h=N_HI),
                    func=ACT.Identity,
                    bias=bias[:, n_buf_rows + c : n_buf_rows + c + 1],
                    scale=1.0,
                )

        def p_passes(half, g):
            for c in range(HALF_CHUNKS * half, HALF_CHUNKS * (half + 1)):
                mx_pass(p_ps[c][:], top_unit[g], P * c, cells_q[g], g == 0, g == CELL_PASSES - 1)

        bias = const.tile([P, n_buf_rows + HID_CHUNKS], F32)
        order_z(0)
        order_z(1)
        transpose_z(0)
        transpose_z(1)
        bias_ps = psum.tile([P, P], BF16, name="bias_ps", tag="bank")
        nc.tensor.transpose(bias_ps[:], bias_rows[:], ident_bf[:])
        regroup(0, "vector")
        regroup(1, "vector")
        regroup(2, "scalar")
        regroup(3, "scalar")
        quantise_z(0)
        quantise(0)
        quantise_z(1)
        quantise(1)
        nc.vector.tensor_copy(out=bias[:], in_=bias_ps[:, 0 : n_buf_rows + HID_CHUNKS])
        buffer_passes(0)
        add_bias(0)
        exponential(0)
        regroup(4, "vector")
        quantise(2)
        regroup(5, "vector")
        quantise(3)
        buffer_passes(1)
        add_bias(1)
        quantise(4)
        quantise(5)
        transpose_cells(0)
        transpose_cells(1)
        buffer_passes(2)
        transpose_cells(2)
        transpose_cells(3)
        group_cells(0)
        exponential(1)
        group_cells(1)
        add_bias(2)
        exponential(2)
        group_cells(2)
        group_cells(3)
        regroup(top_unit[0], "scalar", 0)
        regroup(top_unit[2], "scalar", 0)
        regroup(top_unit[3], "scalar", 0)
        nc.scalar.activation(out=warm[:, 3:4], in_=warm[:, 2:3], func=ACT.Gelu)

        negative_part(0)
        regroup(low_unit[0], "vector", 0)
        finish_elu(0)
        regroup(low_unit[1], "vector", 0)
        quantise_zb(0)
        quantise(low_unit[0], 0)
        quantise(low_unit[1], 0)
        negative_part(1)
        quantise_cells(0)
        finish_elu(1)
        quantise_cells(1)
        regroup(low_unit[2], "vector", 0)
        quantise_zb(1)
        negative_part(2)
        quantise(low_unit[2], 0)
        finish_elu(2)
        regroup(top_unit[1], "vector", 0)
        quantise_zb(2)
        q_passes(0)
        move_q(0)
        quantise_cells(2)
        quantise_cells(3)
        for g in range(CELL_PASSES - 1):
            quantise(top_unit[g], 0)
            p_passes(0, g)
        regroup(low_unit[0], "vector", 1)
        quantise(top_unit[3], 0)
        p_passes(0, 3)
        p_sb = [keep.tile([P, M], F32, name="p_sb%d" % half) for half in range(HALVES)]

        def copy_p(half):
            nc.scalar.copy(out=p_sb[half][:], in_=p_ps[HALF_CHUNKS * half][:])

        copy_p(0)

        out_slots = out.rearrange("b i j h -> (b i) j h")

        def q_of_slots(c, mt, quad):
            return (
                q_sb[:, c, P * mt : P * (mt + 1)]
                .rearrange("p (b j) -> p j b", j=N)[:, QUAD * quad : QUAD * (quad + 1), :]
                .unsqueeze(3)
                .to_broadcast([P, QUAD, TILE_BATCHES, N])
            )

        def sum_on_vector(c, mt, quad):
            sums = stage.tile([P, QUAD, P], F32, name="sums", bufs=8)
            nc.vector.tensor_tensor(
                out=sums[:].rearrange("p j (b i) -> p j b i", i=N),
                in0=p_ps[c][:, P * mt : P * (mt + 1)]
                .rearrange("p (b i) -> p b i", i=N)
                .unsqueeze(1)
                .to_broadcast([P, QUAD, TILE_BATCHES, N]),
                in1=q_of_slots(c, mt, quad),
                op=ALU.add,
            )
            return [sums]

        def sum_on_tensor(c, mt, quad):
            rep = stage.tile([P, QUAD, P], F32, name="rep", bufs=4)
            nc.vector.tensor_copy(out=rep[:].rearrange("p j (b i) -> p j b i", i=N), in_=q_of_slots(c, mt, quad))
            return [p_sb[c // HALF_CHUNKS][:, P * mt : P * (mt + 1)], rep]

        def group_sums(half, grp, first_on_tensor):
            mt, quad = divmod(grp, QUADS)
            sources = []
            for s in range(HALF_CHUNKS):
                c = HALF_CHUNKS * half + s
                if s == 0 and first_on_tensor:
                    sources.append(sum_on_tensor(c, mt, quad))
                else:
                    sources.append(sum_on_vector(c, mt, quad))
            return sources

        def finish_group(half, grp, sources):
            mt, quad = divmod(grp, QUADS)
            o_sb = stage.tile([P, QUAD, HALF_COLS], F32, name="o_sb", bufs=6)
            for pair in range(QUAD // 2):
                o_ps = psum.tile([P, 2, HALF_COLS], F32, name="o_ps", tag="bank")
                for e in range(2):
                    j = 2 * pair + e
                    for s in range(HALF_CHUNKS):
                        parts = sources[s]
                        for n, part in enumerate(parts):
                            nc.tensor.matmul(
                                o_ps[:, e, P * s : P * (s + 1)],
                                lhsT=part[:, j, :] if n == len(parts) - 1 else part,
                                rhs=ident_f32[:],
                                start=(n == 0),
                                stop=(n == len(parts) - 1),
                                is_transpose=True,
                            )
                nc.scalar.activation(out=o_sb[:, 2 * pair : 2 * pair + 2, :], in_=o_ps[:], func=ACT.Gelu)
            nc.sync.dma_start(
                out=out_slots[
                    P * mt : P * (mt + 1), QUAD * quad : QUAD * (quad + 1), HALF_COLS * half : HALF_COLS * (half + 1)
                ],
                in_=o_sb[:],
            )

        def keep_busy():
            busy_ps = psum_p.tile([P, UNIT_COLS], F32, name="busy_ps", tag="p_ps0")
            nc.tensor.matmul(busy_ps[:], lhsT=ident_bf[:], rhs=raw_units[0][:, 0, :], start=True, stop=True)

        for grp in range(M_TILES * QUADS):
            finish_group(0, grp, group_sums(0, grp, True))
            if grp not in (2, 5, 6):
                keep_busy()
            if grp == 1:
                regroup(top_unit[2], "scalar", 1)
                regroup(low_unit[1], "vector", 1)
                regroup(low_unit[2], "vector", 1)
                quantise(low_unit[0], 1)
            elif grp == 2:
                quantise(low_unit[1], 1)
                quantise(low_unit[2], 1)
                q_passes(1)
            elif grp == 3:
                move_q(1)
                regroup(top_unit[0], "vector", 1)
                regroup(top_unit[1], "vector", 1)
            elif grp == 4:
                quantise(top_unit[0], 1)
                quantise(top_unit[1], 1)
            elif grp == 5:
                p_passes(1, 0)
                p_passes(1, 1)
                regroup(top_unit[3], "vector", 1)
                quantise(top_unit[2], 1)
            elif grp == 6:
                quantise(top_unit[3], 1)
                p_passes(1, 2)
                p_passes(1, 3)
        for grp in range(M_TILES * QUADS):
            sources = group_sums(1, grp, grp % 2 == 1)
            if grp == 0:
                copy_p(1)
            finish_group(1, grp, sources)
            if grp in (1, 3, 5):
                keep_busy()
